import numpy as np
import ml_dtypes


def mxq(x, axis, fmt="e4m3"):
    dtype, down = {"e4m3": (ml_dtypes.float8_e4m3fn, 7), "e5m2": (ml_dtypes.float8_e5m2, 14)}[fmt]
    v = np.moveaxis(np.asarray(x, np.float32).astype(ml_dtypes.bfloat16).astype(np.float64), axis, -1)
    blocks = v.reshape(v.shape[:-1] + (-1, 32))
    amax = np.abs(blocks).max(-1, keepdims=True)
    byte = np.maximum(np.where(amax > 0, np.frexp(amax)[1] - 1 + 127, 0) - down, 1)
    scale = np.exp2(byte - 127.0)
    codes = (blocks / scale).astype(np.float32).astype(dtype).astype(np.float64)
    return np.moveaxis((codes * scale).reshape(v.shape), -1, axis)


WIDE = False


def mx_kscale(k):
    if not WIDE:
        return np.ones(k)
    levels = np.array([10, -10, 5, -5, 0])
    a = np.random.permutation(np.resize(levels, k // 512 * 4)).reshape(k // 512, 4)
    idx = np.arange(k)
    return np.exp2(a[idx // 512, idx % 128 // 32])


BF16 = ml_dtypes.bfloat16


def bf(x):
    return np.asarray(x, np.float32).astype(BF16)


def f64(x):
    return np.asarray(x).astype(np.float64)


E2M1 = np.array([0.0, 0.5, 1.0, 1.5, 2.0, 3.0, 4.0, 6.0, -0.0, -0.5, -1.0, -1.5, -2.0, -3.0, -4.0, -6.0])


def pack_weight(w, fmt):
    k, n = w.shape
    w = f64(bf(w)).reshape(k // 32, 32, n)
    amax = np.abs(w).max(1)
    if fmt == "e4m3":
        byte = np.frexp(amax)[1] - 1 + 127 - 7
    else:
        mant, ex = np.frexp(amax / 6.0)
        byte = np.where(mant > 0.5, ex, ex - 1) + 127
    byte = np.clip(np.where(amax > 0, byte, 1), 1, 254)
    scaled = (w * np.exp2(127.0 - byte)[:, None, :]).reshape(k, n).astype(np.float32)
    by_word = np.ascontiguousarray(scaled.reshape(k // 512, 128, 4, n).transpose(0, 1, 3, 2))
    if fmt == "e4m3":
        words = by_word.astype(ml_dtypes.float8_e4m3fn).view(np.uint8)
    else:
        c = by_word.astype(ml_dtypes.float4_e2m1fn).view(np.uint8) & 0xF
        words = c[..., 0::2] | (c[..., 1::2] << 4)
    return np.ascontiguousarray(words), np.ascontiguousarray(byte.astype(np.uint8).reshape(k // 512, 16, n))


def unpack_weight(words, scales, fmt):
    g, p, n, _ = words.shape
    if fmt == "e4m3":
        vals = np.ascontiguousarray(words).view(ml_dtypes.float8_e4m3fn).astype(np.float64)
    else:
        nib = np.empty((g, p, n, 4), np.uint8)
        nib[..., 0::2] = words & 0xF
        nib[..., 1::2] = words >> 4
        vals = E2M1[nib]
    vals = vals * np.repeat(np.exp2(scales.astype(np.float64) - 127.0), 8, axis=1)[..., None]
    return vals.transpose(0, 1, 3, 2).reshape(g * 512, n)


B, L, D, C = 128, 20, 512, 512
T1, T2, T3 = 1, 2, 3
EPS = 1e-12
FMT = "e4m3"


def conv_relu(xq, wq, b):
    k = wq.shape[0]
    n = xq.shape[1]
    out = b
    for j in range(k):
        out = out + (xq[:, j:n - k + 1 + j] @ wq[j])
    return np.maximum(out, 0.0)


def l2norm(x, axis):
    n = np.sqrt(np.sum(x * x, axis=axis, keepdims=True))
    return x / np.maximum(n, EPS)


def setup_inputs():
    s = mx_kscale(D)

    def wdraw(k):
        stack = np.random.standard_normal((k, D, C)) / np.sqrt(k * D) / s[None, :, None]
        return pack_weight(stack.reshape(-1, C), FMT)

    words_emb = bf(np.random.standard_normal((B, L, D)) * s)
    W1_words, W1_scales = wdraw(T1)
    b1 = bf(np.random.standard_normal(C) * 0.3)
    W2_words, W2_scales = wdraw(T2)
    b2 = bf(np.random.standard_normal(C) * 0.3)
    W3_words, W3_scales = wdraw(T3)
    b3 = bf(np.random.standard_normal(C) * 0.3)
    return {"words_emb": words_emb,
            "W1_words": W1_words, "W1_scales": W1_scales, "b1": b1,
            "W2_words": W2_words, "W2_scales": W2_scales, "b2": b2,
            "W3_words": W3_words, "W3_scales": W3_scales, "b3": b3}


def reference(words_emb, W1_words, W1_scales, b1, W2_words, W2_scales, b2, W3_words, W3_scales, b3):
    xq = mxq(f64(words_emb), 2, "e4m3")
    a = conv_relu(xq, unpack_weight(W1_words, W1_scales, FMT).reshape(T1, D, C), f64(b1))
    b_ = conv_relu(xq, unpack_weight(W2_words, W2_scales, FMT).reshape(T2, D, C), f64(b2))
    c = conv_relu(xq, unpack_weight(W3_words, W3_scales, FMT).reshape(T3, D, C), f64(b3))
    b_pad = np.pad(b_, ((0, 0), (0, L - b_.shape[1]), (0, 0)))
    c_pad = np.pad(c, ((0, 0), (0, L - c.shape[1]), (0, 0)))
    code = np.maximum(np.maximum(a, b_pad), c_pad)
    code = l2norm(code, 2)
    words_out = np.transpose(code, (0, 2, 1))
    pooled = (a.max(axis=1) + b_.max(axis=1) + c.max(axis=1)) / 3.0
    return (words_out, pooled)

@@ -1,0 +1,269 @@
+from contextlib import ExitStack
+
+import concourse.mybir as mybir
+from concourse.masks import make_identity
+
+F32 = mybir.dt.float32
+BF16 = mybir.dt.bfloat16
+I32 = mybir.dt.int32
+U32 = mybir.dt.uint32
+U8 = mybir.dt.uint8
+FP8X4 = mybir.dt.float8_e4m3fn_x4
+ALU = mybir.AluOpType
+FUNC = mybir.ActivationFunctionType
+
+P = 128
+SENTENCES = 128
+POSITIONS = 20
+EMBED = 512
+FEATURES = 512
+WIDTHS = (1, 2, 3)
+FIRST_TAP = {1: 0, 2: 1, 3: 3}
+TAPS = sum(WIDTHS)
+CHUNKS = FEATURES // P
+GROUP = 4
+GROUPS = POSITIONS // GROUP
+PAD = max(WIDTHS) - 1
+EPS = 1e-12
+
+FLOPS = 2 * SENTENCES * EMBED * FEATURES * sum(k * (POSITIONS - k + 1) for k in WIDTHS)
+
+
+def tokens(first_position, count):
+    return slice(first_position * SENTENCES, (first_position + count) * SENTENCES)
+
+
+def positions_in_group(width, group):
+    return min(GROUP, POSITIONS - width + 1 - group * GROUP)
+
+
+def tile_bertheading_pa_e_kernel(
+    tc, words_emb, W1_words, W1_scales, b1, W2_words, W2_scales, b2, W3_words, W3_scales, b3, words_out, pooled
+):
+    nc = tc.nc
+    weight_words = {1: W1_words, 2: W2_words, 3: W3_words}
+    weight_scales = {1: W1_scales, 2: W2_scales, 3: W3_scales}
+    biases = {1: b1, 2: b2, 3: b3}
+
+    with ExitStack() as ctx:
+        keep = ctx.enter_context(tc.tile_pool(name="keep", bufs=1))
+        stage = ctx.enter_context(tc.tile_pool(name="stage", bufs=2))
+        small = ctx.enter_context(tc.tile_pool(name="small", bufs=2))
+        scratch = ctx.enter_context(tc.tile_pool(name="scratch", bufs=GROUP))
+        conv_banks = ctx.enter_context(tc.psum_pool(name="conv_banks", bufs=4))
+        flip_banks = ctx.enter_context(tc.psum_pool(name="flip_banks", bufs=4))
+
+        x_sb = keep.tile([P, POSITIONS, EMBED], BF16, name="x_sb")
+        x_codes = keep.tile([P, (POSITIONS + PAD) * SENTENCES], U32, name="x_codes", align_bytes=64)
+        x_scales = keep.tile([P, (POSITIONS + PAD) * SENTENCES], U8, name="x_scales", align_bytes=64)
+        w_codes = keep.tile([P, TAPS, FEATURES], U32, name="w_codes", align_bytes=64)
+        w_scales = keep.tile([P, TAPS, FEATURES], U8, name="w_scales", align_bytes=64)
+        identity = keep.tile([P, P], F32, name="identity")
+        bias_rows = keep.tile([P, P], BF16, name="bias_rows")
+        bias_rows_f32 = keep.tile([P, P], F32, name="bias_rows_f32")
+        bias_cols = keep.tile([P, len(WIDTHS) * CHUNKS], F32, name="bias_cols")
+        table_warmer = keep.tile([P, 1], F32, name="table_warmer")
+        conv1 = keep.tile([P, CHUNKS, POSITIONS * SENTENCES], F32, name="conv1")
+        best = {
+            2: keep.tile([P, CHUNKS, GROUP * SENTENCES], F32, name="best2"),
+            3: keep.tile([P, CHUNKS, GROUP * SENTENCES], F32, name="best3"),
+        }
+        pooled_sum = keep.tile([P, CHUNKS, SENTENCES], F32, name="pooled_sum")
+        pooled_sb = keep.tile([P, FEATURES], F32, name="pooled_sb")
+        out_sb = keep.tile([P, FEATURES, POSITIONS], F32, name="out_sb")
+
+        nc.vector.memset(w_scales[:].bitcast(I32), 0)
+        nc.vector.memset(x_codes[:, tokens(POSITIONS, PAD)].bitcast(I32), 0)
+        nc.vector.memset(x_scales[:, tokens(POSITIONS, PAD)].bitcast(I32), 0)
+        nc.vector.memset(bias_rows[:], 0.0)
+        nc.vector.memset(table_warmer[:], 1.0)
+        nc.scalar.sqrt(table_warmer[:], table_warmer[:])
+        make_identity(nc, identity[:])
+
+        def load_positions(group):
+            span = slice(group * GROUP, (group + 1) * GROUP)
+            nc.sync.dma_start(out=x_sb[:, span, :], in_=words_emb[:, span, :])
+
+        def load_weight(width):
+            first = FIRST_TAP[width]
+            for tap in range(width):
+                nc.sync.dma_start(
+                    out=w_codes[:, first + tap, :].bitcast(I32),
+                    in_=weight_words[width][tap].rearrange("q n t -> q (n t)").bitcast(I32),
+                )
+            for quadrant in range(4):
+                nc.sync.dma_start(
+                    out=w_scales[32 * quadrant : 32 * quadrant + 4, first : first + width, :].bitcast(I32),
+                    in_=weight_scales[width][:, 4 * quadrant : 4 * quadrant + 4, :]
+                    .rearrange("g r n -> r g n")
+                    .bitcast(I32),
+                )
+
+        for width in WIDTHS:
+            row = (width - 1) * CHUNKS
+            nc.scalar.dma_start(
+                out=bias_rows[row : row + CHUNKS, :], in_=biases[width].rearrange("(r c) -> r c", c=P)
+            )
+        load_positions(0)
+        load_positions(1)
+        for width in WIDTHS:
+            load_weight(width)
+        for group in range(2, GROUPS):
+            load_positions(group)
+
+        nc.vector.tensor_copy(out=bias_rows_f32[:], in_=bias_rows[:])
+        bias_flip = flip_banks.tile([P, FEATURES], F32, tag="flip")
+        nc.tensor.transpose(bias_flip[:, :P], bias_rows_f32[:], identity[:])
+        nc.vector.tensor_copy(out=bias_cols[:], in_=bias_flip[:, : len(WIDTHS) * CHUNKS])
+
+        def bias_of(width, chunk):
+            column = (width - 1) * CHUNKS + chunk
+            return bias_cols[:, column : column + 1]
+
+        def quantise_positions(group):
+            grouped = stage.tile([P, GROUP, SENTENCES, 4], BF16, tag="grouped", align_bytes=64)
+            for pair in range(GROUP // 2):
+                flipped = flip_banks.tile([P, 2, 2, SENTENCES], F32, tag="flip")
+                for i in range(2):
+                    words = x_sb[:, group * GROUP + 2 * pair + i, :].bitcast(F32)
+                    for u in range(2):
+                        nc.tensor.transpose(flipped[:, i, u, :], words[:, u : EMBED // 2 : 2], identity[:])
+                nc.scalar.copy(
+                    out=grouped[:, 2 * pair : 2 * pair + 2, :, :].bitcast(F32),
+                    in_=flipped[:].rearrange("q i u n -> q i n u"),
+                )
+            here = tokens(group * GROUP, GROUP)
+            nc.vector.quantize_mx(
+                out=x_codes[:, here].bitcast(FP8X4),
+                scales=x_scales[:, here],
+                in_=grouped[:].rearrange("q i n t -> q (i n t)"),
+            )
+
+        def convolve(width, group, chunk):
+            bank = conv_banks.tile([P, GROUP * SENTENCES], F32, tag="conv")
+            features = slice(chunk * P, (chunk + 1) * P)
+            for tap in range(width):
+                shifted = tokens(group * GROUP + tap, GROUP)
+                nc.tensor.matmul_mx(
+                    out=bank[:],
+                    lhsT=w_codes[:, FIRST_TAP[width] + tap, features].bitcast(FP8X4),
+                    lhsT_scale=w_scales[:, FIRST_TAP[width] + tap, features],
+                    rhs=x_codes[:, shifted].bitcast(FP8X4),
+                    rhs_scale=x_scales[:, shifted],
+                    start=(tap == 0),
+                    stop=(tap == width - 1),
+                )
+            return bank
+
+        def convolve_and_fold(group, chunk, code):
+            banks = {}
+            for width in WIDTHS:
+                banks[width] = convolve(width, group, chunk)
+            nc.scalar.activation(
+                out=conv1[:, chunk, tokens(group * GROUP, GROUP)],
+                in_=banks[1][:],
+                func=FUNC.Relu,
+                bias=bias_of(1, chunk),
+                scale=1.0,
+            )
+            for width in (2, 3):
+                count = positions_in_group(width, group)
+                cols = tokens(0, count)
+                so_far = conv1[:, chunk, tokens(group * GROUP, count)] if width == 2 else code[:, chunk, cols]
+                if group == 0:
+                    nc.scalar.activation(
+                        out=best[width][:, chunk, :],
+                        in_=banks[width][:],
+                        func=FUNC.Relu,
+                        bias=bias_of(width, chunk),
+                        scale=1.0,
+                    )
+                    nc.vector.tensor_max(code[:, chunk, cols], best[width][:, chunk, cols], so_far)
+                else:
+                    nc.vector.scalar_tensor_tensor(
+                        out=code[:, chunk, cols],
+                        in0=banks[width][:, cols],
+                        scalar=bias_of(width, chunk),
+                        in1=so_far,
+                        op0=ALU.add,
+                        op1=ALU.max,
+                    )
+                    nc.vector.scalar_tensor_tensor(
+                        out=best[width][:, chunk, cols],
+                        in0=banks[width][:, cols],
+                        scalar=bias_of(width, chunk),
+                        in1=best[width][:, chunk, cols],
+                        op0=ALU.add,
+                        op1=ALU.max,
+                    )
+
+        def normalise(group, code):
+            sum_squares = small.tile([P, GROUP], F32, tag="sum_squares")
+            norm = small.tile([P, GROUP], F32, tag="norm")
+            inverse = small.tile([P, GROUP], F32, tag="inverse")
+            scaled = stage.tile([P, GROUP, FEATURES], F32, tag="scaled")
+            flipped = []
+            for i in range(GROUP):
+                position = group * GROUP + i
+                by_sentence = flip_banks.tile([P, FEATURES], F32, tag="flip", name="by_sentence")
+                for chunk in range(CHUNKS):
+                    if i < positions_in_group(2, group):
+                        source = code[:, chunk, tokens(i, 1)]
+                    else:
+                        source = conv1[:, chunk, tokens(position, 1)]
+                    nc.tensor.transpose(by_sentence[:, chunk * P : (chunk + 1) * P], source, identity[:])
+                squares = scratch.tile([P, FEATURES], BF16, tag="squares")
+                nc.scalar.activation(
+                    out=squares[:], in_=by_sentence[:], func=FUNC.Square, accum_out=sum_squares[:, i : i + 1]
+                )
+                flipped.append(by_sentence)
+            nc.vector.tensor_scalar_max(norm[:], sum_squares[:], EPS * EPS)
+            nc.scalar.sqrt(norm[:], norm[:])
+            nc.vector.reciprocal(inverse[:], norm[:])
+            for i in range(GROUP):
+                nc.scalar.activation(
+                    out=scaled[:, i, :], in_=flipped[i][:], func=FUNC.Copy, scale=inverse[:, i : i + 1]
+                )
+            for chunk in range(CHUNKS):
+                features = slice(chunk * P, (chunk + 1) * P)
+                nc.gpsimd.tensor_scalar(
+                    out=out_sb[:, features, group * GROUP : (group + 1) * GROUP],
+                    in0=scaled[:, :, features].rearrange("n i c -> n c i"),
+                    scalar1=1.0,
+                    scalar2=0.0,
+                    op0=ALU.mult,
+                    op1=ALU.add,
+                )
+                if group == GROUPS - 1:
+                    nc.sync.dma_start(out=words_out[:, features, :], in_=out_sb[:, features, :])
+
+        def max_over_positions(row, count):
+            while count > 1:
+                half = count // 2
+                nc.vector.tensor_max(row[:, tokens(0, half)], row[:, tokens(0, half)], row[:, tokens(count - half, half)])
+                count -= half
+
+        quantise_positions(0)
+        quantise_positions(1)
+        codes = {}
+        for group in range(GROUPS):
+            codes[group] = stage.tile([P, CHUNKS, GROUP * SENTENCES], F32, tag="code", name="code")
+            for chunk in range(CHUNKS):
+                convolve_and_fold(group, chunk, codes[group])
+                if chunk == 0 and group + 2 < GROUPS:
+                    quantise_positions(group + 2)
+                if chunk == 1 and group > 0:
+                    normalise(group - 1, codes[group - 1])
+        normalise(GROUPS - 1, codes[GROUPS - 1])
+
+        pooled_flip = flip_banks.tile([P, FEATURES], F32, tag="flip")
+        first = tokens(0, 1)
+        for chunk in range(CHUNKS):
+            max_over_positions(conv1[:, chunk, :], POSITIONS)
+            max_over_positions(best[2][:, chunk, :], GROUP)
+            max_over_positions(best[3][:, chunk, :], GROUP)
+            nc.vector.tensor_add(pooled_sum[:, chunk, :], conv1[:, chunk, first], best[2][:, chunk, first])
+            nc.vector.tensor_add(pooled_sum[:, chunk, :], pooled_sum[:, chunk, :], best[3][:, chunk, first])
+            nc.tensor.transpose(pooled_flip[:, chunk * P : (chunk + 1) * P], pooled_sum[:, chunk, :], identity[:])
+        nc.scalar.activation(out=pooled_sb[:], in_=pooled_flip[:], func=FUNC.Copy, scale=1.0 / len(WIDTHS))
+        nc.sync.dma_start(out=pooled[:, :], in_=pooled_sb[:])

@@ -11,6 +11,7 @@ U8 = mybir.dt.uint8
 FP8X4 = mybir.dt.float8_e4m3fn_x4
 ALU = mybir.AluOpType
 FUNC = mybir.ActivationFunctionType
+INNERMOST = mybir.AxisListType.X
 
 P = 128
 SENTENCES = 128
@@ -23,7 +24,7 @@ TAPS = sum(WIDTHS)
 CHUNKS = FEATURES // P
 GROUP = 4
 GROUPS = POSITIONS // GROUP
-PAD = max(WIDTHS) - 1
+AHEAD = 2
 EPS = 1e-12
 
 FLOPS = 2 * SENTENCES * EMBED * FEATURES * sum(k * (POSITIONS - k + 1) for k in WIDTHS)
@@ -37,6 +38,16 @@ def positions_in_group(width, group):
     return min(GROUP, POSITIONS - width + 1 - group * GROUP)
 
 
+def moving_pieces(count):
+    pieces = []
+    first = 0
+    for size in (4, 2, 1):
+        if count - first >= size:
+            pieces.append((first, size))
+            first += size
+    return pieces
+
+
 def tile_bertheading_pa_e_kernel(
     tc, words_emb, W1_words, W1_scales, b1, W2_words, W2_scales, b2, W3_words, W3_scales, b3, words_out, pooled
 ):
@@ -46,54 +57,52 @@ def tile_bertheading_pa_e_kernel(
     biases = {1: b1, 2: b2, 3: b3}
 
     with ExitStack() as ctx:
+        ctx.enter_context(tc.manual_schedule())
         keep = ctx.enter_context(tc.tile_pool(name="keep", bufs=1))
         stage = ctx.enter_context(tc.tile_pool(name="stage", bufs=2))
-        small = ctx.enter_context(tc.tile_pool(name="small", bufs=2))
-        scratch = ctx.enter_context(tc.tile_pool(name="scratch", bufs=GROUP))
         conv_banks = ctx.enter_context(tc.psum_pool(name="conv_banks", bufs=4))
         flip_banks = ctx.enter_context(tc.psum_pool(name="flip_banks", bufs=4))
 
         x_sb = keep.tile([P, POSITIONS, EMBED], BF16, name="x_sb")
-        x_codes = keep.tile([P, (POSITIONS + PAD) * SENTENCES], U32, name="x_codes", align_bytes=64)
-        x_scales = keep.tile([P, (POSITIONS + PAD) * SENTENCES], U8, name="x_scales", align_bytes=64)
+        x_codes = keep.tile([P, POSITIONS * SENTENCES], U32, name="x_codes", align_bytes=64)
+        x_scales = keep.tile([P, POSITIONS * SENTENCES], U8, name="x_scales", align_bytes=64)
         w_codes = keep.tile([P, TAPS, FEATURES], U32, name="w_codes", align_bytes=64)
         w_scales = keep.tile([P, TAPS, FEATURES], U8, name="w_scales", align_bytes=64)
         identity = keep.tile([P, P], F32, name="identity")
+        minus_half = keep.tile([P, GROUP], F32, name="minus_half")
         bias_rows = keep.tile([P, P], BF16, name="bias_rows")
         bias_rows_f32 = keep.tile([P, P], F32, name="bias_rows_f32")
         bias_cols = keep.tile([P, len(WIDTHS) * CHUNKS], F32, name="bias_cols")
-        table_warmer = keep.tile([P, 1], F32, name="table_warmer")
         conv1 = keep.tile([P, CHUNKS, POSITIONS * SENTENCES], F32, name="conv1")
         best = {
             2: keep.tile([P, CHUNKS, GROUP * SENTENCES], F32, name="best2"),
             3: keep.tile([P, CHUNKS, GROUP * SENTENCES], F32, name="best3"),
         }
-        pooled_sum = keep.tile([P, CHUNKS, SENTENCES], F32, name="pooled_sum")
+        conv1_fifths = keep.tile([P, CHUNKS, GROUPS * SENTENCES], F32, name="conv1_fifths")
+        top = {}
+        for width in WIDTHS:
+            top[width] = keep.tile([P, CHUNKS, SENTENCES], F32, name="top%d" % width)
         pooled_sb = keep.tile([P, FEATURES], F32, name="pooled_sb")
         out_sb = keep.tile([P, FEATURES, POSITIONS], F32, name="out_sb")
 
         nc.vector.memset(w_scales[:].bitcast(I32), 0)
-        nc.vector.memset(x_codes[:, tokens(POSITIONS, PAD)].bitcast(I32), 0)
-        nc.vector.memset(x_scales[:, tokens(POSITIONS, PAD)].bitcast(I32), 0)
         nc.vector.memset(bias_rows[:], 0.0)
-        nc.vector.memset(table_warmer[:], 1.0)
-        nc.scalar.sqrt(table_warmer[:], table_warmer[:])
         make_identity(nc, identity[:])
+        nc.gpsimd.memset(minus_half[:], -0.5)
 
         def load_positions(group):
             span = slice(group * GROUP, (group + 1) * GROUP)
             nc.sync.dma_start(out=x_sb[:, span, :], in_=words_emb[:, span, :])
 
         def load_weight(width):
-            first = FIRST_TAP[width]
-            for tap in range(width):
-                nc.sync.dma_start(
-                    out=w_codes[:, first + tap, :].bitcast(I32),
-                    in_=weight_words[width][tap].rearrange("q n t -> q (n t)").bitcast(I32),
-                )
+            taps = slice(FIRST_TAP[width], FIRST_TAP[width] + width)
+            nc.sync.dma_start(
+                out=w_codes[:, taps, :].bitcast(I32),
+                in_=weight_words[width].rearrange("g q n t -> q g (n t)").bitcast(I32),
+            )
             for quadrant in range(4):
                 nc.sync.dma_start(
-                    out=w_scales[32 * quadrant : 32 * quadrant + 4, first : first + width, :].bitcast(I32),
+                    out=w_scales[32 * quadrant : 32 * quadrant + 4, taps, :].bitcast(I32),
                     in_=weight_scales[width][:, 4 * quadrant : 4 * quadrant + 4, :]
                     .rearrange("g r n -> r g n")
                     .bitcast(I32),
@@ -101,58 +110,48 @@ def tile_bertheading_pa_e_kernel(
 
         for width in WIDTHS:
             row = (width - 1) * CHUNKS
-            nc.scalar.dma_start(
+            nc.gpsimd.dma_start(
                 out=bias_rows[row : row + CHUNKS, :], in_=biases[width].rearrange("(r c) -> r c", c=P)
             )
-        load_positions(0)
-        load_positions(1)
+        for group in range(AHEAD):
+            load_positions(group)
         for width in WIDTHS:
             load_weight(width)
-        for group in range(2, GROUPS):
+        for group in range(AHEAD, GROUPS):
             load_positions(group)
-
-        nc.vector.tensor_copy(out=bias_rows_f32[:], in_=bias_rows[:])
-        bias_flip = flip_banks.tile([P, FEATURES], F32, tag="flip")
-        nc.tensor.transpose(bias_flip[:, :P], bias_rows_f32[:], identity[:])
-        nc.vector.tensor_copy(out=bias_cols[:], in_=bias_flip[:, : len(WIDTHS) * CHUNKS])
 
         def bias_of(width, chunk):
             column = (width - 1) * CHUNKS + chunk
             return bias_cols[:, column : column + 1]
 
-        def quantise_positions(group):
-            grouped = stage.tile([P, GROUP, SENTENCES, 4], BF16, tag="grouped", align_bytes=64)
-            for pair in range(GROUP // 2):
-                flipped = flip_banks.tile([P, 2, 2, SENTENCES], F32, tag="flip")
-                for i in range(2):
-                    words = x_sb[:, group * GROUP + 2 * pair + i, :].bitcast(F32)
-                    for u in range(2):
-                        nc.tensor.transpose(flipped[:, i, u, :], words[:, u : EMBED // 2 : 2], identity[:])
-                nc.scalar.copy(
-                    out=grouped[:, 2 * pair : 2 * pair + 2, :, :].bitcast(F32),
-                    in_=flipped[:].rearrange("q i u n -> q i n u"),
-                )
-            here = tokens(group * GROUP, GROUP)
+        def quantise_position(position):
+            words = x_sb[:, position, :].bitcast(F32)
+            flipped = flip_banks.tile([P, 2, SENTENCES], F32, tag="flip")
+            for u in range(2):
+                nc.tensor.transpose(flipped[:, u, :], words[:, u : EMBED // 2 : 2], identity[:])
+            grouped = stage.tile([P, SENTENCES, 4], BF16, tag="grouped", align_bytes=64)
+            nc.scalar.copy(out=grouped[:].bitcast(F32), in_=flipped[:].rearrange("q u n -> q n u"))
             nc.vector.quantize_mx(
-                out=x_codes[:, here].bitcast(FP8X4),
-                scales=x_scales[:, here],
-                in_=grouped[:].rearrange("q i n t -> q (i n t)"),
+                out=x_codes[:, tokens(position, 1)].bitcast(FP8X4),
+                scales=x_scales[:, tokens(position, 1)],
+                in_=grouped[:].rearrange("q n t -> q (n t)"),
             )
 
         def convolve(width, group, chunk):
             bank = conv_banks.tile([P, GROUP * SENTENCES], F32, tag="conv")
             features = slice(chunk * P, (chunk + 1) * P)
-            for tap in range(width):
-                shifted = tokens(group * GROUP + tap, GROUP)
-                nc.tensor.matmul_mx(
-                    out=bank[:],
-                    lhsT=w_codes[:, FIRST_TAP[width] + tap, features].bitcast(FP8X4),
-                    lhsT_scale=w_scales[:, FIRST_TAP[width] + tap, features],
-                    rhs=x_codes[:, shifted].bitcast(FP8X4),
-                    rhs_scale=x_scales[:, shifted],
-                    start=(tap == 0),
-                    stop=(tap == width - 1),
-                )
+            for first, size in moving_pieces(positions_in_group(width, group)):
+                for tap in range(width):
+                    shifted = tokens(group * GROUP + first + tap, size)
+                    nc.tensor.matmul_mx(
+                        out=bank[:, tokens(first, size)],
+                        lhsT=w_codes[:, FIRST_TAP[width] + tap, features].bitcast(FP8X4),
+                        lhsT_scale=w_scales[:, FIRST_TAP[width] + tap, features],
+                        rhs=x_codes[:, shifted].bitcast(FP8X4),
+                        rhs_scale=x_scales[:, shifted],
+                        start=(tap == 0),
+                        stop=(tap == width - 1),
+                    )
             return bank
 
         def convolve_and_fold(group, chunk, code):
@@ -197,73 +196,84 @@ def tile_bertheading_pa_e_kernel(
                         op1=ALU.max,
                     )
 
-        def normalise(group, code):
-            sum_squares = small.tile([P, GROUP], F32, tag="sum_squares")
-            norm = small.tile([P, GROUP], F32, tag="norm")
-            inverse = small.tile([P, GROUP], F32, tag="inverse")
-            scaled = stage.tile([P, GROUP, FEATURES], F32, tag="scaled")
-            flipped = []
-            for i in range(GROUP):
-                position = group * GROUP + i
-                by_sentence = flip_banks.tile([P, FEATURES], F32, tag="flip", name="by_sentence")
-                for chunk in range(CHUNKS):
-                    if i < positions_in_group(2, group):
-                        source = code[:, chunk, tokens(i, 1)]
-                    else:
-                        source = conv1[:, chunk, tokens(position, 1)]
-                    nc.tensor.transpose(by_sentence[:, chunk * P : (chunk + 1) * P], source, identity[:])
-                squares = scratch.tile([P, FEATURES], BF16, tag="squares")
-                nc.scalar.activation(
-                    out=squares[:], in_=by_sentence[:], func=FUNC.Square, accum_out=sum_squares[:, i : i + 1]
-                )
-                flipped.append(by_sentence)
-            nc.vector.tensor_scalar_max(norm[:], sum_squares[:], EPS * EPS)
-            nc.scalar.sqrt(norm[:], norm[:])
-            nc.vector.reciprocal(inverse[:], norm[:])
-            for i in range(GROUP):
-                nc.scalar.activation(
-                    out=scaled[:, i, :], in_=flipped[i][:], func=FUNC.Copy, scale=inverse[:, i : i + 1]
-                )
+        def flip_position(group, i, code, by_sentence, sum_squares):
+            flipped = flip_banks.tile([P, FEATURES], F32, tag="flip")
+            for chunk in range(CHUNKS):
+                if i < positions_in_group(2, group):
+                    source = code[:, chunk, tokens(i, 1)]
+                else:
+                    source = conv1[:, chunk, tokens(group * GROUP + i, 1)]
+                nc.tensor.transpose(flipped[:, chunk * P : (chunk + 1) * P], source, identity[:])
+            squares = stage.tile([P, FEATURES], BF16, tag="squares")
+            nc.scalar.activation(out=squares[:], in_=flipped[:], func=FUNC.Square, accum_out=sum_squares[:, i : i + 1])
+            nc.scalar.copy(out=by_sentence[:, i, :], in_=flipped[:])
+
+        def normalise(group, by_sentence, sum_squares):
+            inverse = stage.tile([P, GROUP], F32, tag="inverse")
+            nc.gpsimd.tensor_scalar_max(inverse[:], sum_squares[:], EPS * EPS)
+            nc.gpsimd.tensor_tensor(out=inverse[:], in0=inverse[:], in1=minus_half[:], op=ALU.pow)
             for chunk in range(CHUNKS):
                 features = slice(chunk * P, (chunk + 1) * P)
-                nc.gpsimd.tensor_scalar(
+                nc.gpsimd.tensor_tensor(
                     out=out_sb[:, features, group * GROUP : (group + 1) * GROUP],
-                    in0=scaled[:, :, features].rearrange("n i c -> n c i"),
-                    scalar1=1.0,
-                    scalar2=0.0,
-                    op0=ALU.mult,
-                    op1=ALU.add,
+                    in0=by_sentence[:, :, features].rearrange("n i c -> n c i"),
+                    in1=inverse[:].unsqueeze(1).to_broadcast([P, P, GROUP]),
+                    op=ALU.mult,
                 )
                 if group == GROUPS - 1:
                     nc.sync.dma_start(out=words_out[:, features, :], in_=out_sb[:, features, :])
 
-        def max_over_positions(row, count):
-            while count > 1:
-                half = count // 2
-                nc.vector.tensor_max(row[:, tokens(0, half)], row[:, tokens(0, half)], row[:, tokens(count - half, half)])
-                count -= half
+        for position in range(AHEAD * GROUP):
+            quantise_position(position)
 
-        quantise_positions(0)
-        quantise_positions(1)
-        codes = {}
+        nc.vector.tensor_copy(out=bias_rows_f32[:], in_=bias_rows[:])
+        bias_flip = flip_banks.tile([P, P], F32, tag="flip")
+        nc.tensor.transpose(bias_flip[:], bias_rows_f32[:], identity[:])
+        nc.vector.tensor_copy(out=bias_cols[:], in_=bias_flip[:, : len(WIDTHS) * CHUNKS])
+
+        code = {}
+        by_sentence = {}
+        sum_squares = {}
         for group in range(GROUPS):
-            codes[group] = stage.tile([P, CHUNKS, GROUP * SENTENCES], F32, tag="code", name="code")
-            for chunk in range(CHUNKS):
-                convolve_and_fold(group, chunk, codes[group])
-                if chunk == 0 and group + 2 < GROUPS:
-                    quantise_positions(group + 2)
-                if chunk == 1 and group > 0:
-                    normalise(group - 1, codes[group - 1])
-        normalise(GROUPS - 1, codes[GROUPS - 1])
+            code[group] = stage.tile([P, CHUNKS, GROUP * SENTENCES], F32, tag="code", name="code")
+            by_sentence[group] = stage.tile([P, GROUP, FEATURES], F32, tag="by_sentence", name="by_sentence")
+            sum_squares[group] = stage.tile([P, GROUP], F32, tag="sum_squares", name="sum_squares")
+            for step in range(CHUNKS):
+                convolve_and_fold(group, step, code[group])
+                if group > 0:
+                    flip_position(group - 1, step, code[group - 1], by_sentence[group - 1], sum_squares[group - 1])
+                if group + AHEAD < GROUPS:
+                    quantise_position((group + AHEAD) * GROUP + step)
+            if group > 0:
+                normalise(group - 1, by_sentence[group - 1], sum_squares[group - 1])
+        last = GROUPS - 1
+        for i in range(GROUP):
+            flip_position(last, i, code[last], by_sentence[last], sum_squares[last])
+        normalise(last, by_sentence[last], sum_squares[last])
 
         pooled_flip = flip_banks.tile([P, FEATURES], F32, tag="flip")
-        first = tokens(0, 1)
         for chunk in range(CHUNKS):
-            max_over_positions(conv1[:, chunk, :], POSITIONS)
-            max_over_positions(best[2][:, chunk, :], GROUP)
-            max_over_positions(best[3][:, chunk, :], GROUP)
-            nc.vector.tensor_add(pooled_sum[:, chunk, :], conv1[:, chunk, first], best[2][:, chunk, first])
-            nc.vector.tensor_add(pooled_sum[:, chunk, :], pooled_sum[:, chunk, :], best[3][:, chunk, first])
-            nc.tensor.transpose(pooled_flip[:, chunk * P : (chunk + 1) * P], pooled_sum[:, chunk, :], identity[:])
+            nc.vector.tensor_reduce(
+                out=conv1_fifths[:, chunk, :].rearrange("c (j n) -> c j n", n=SENTENCES),
+                in_=conv1[:, chunk, :].rearrange("c (i j n) -> c j n i", i=GROUP, n=SENTENCES),
+                axis=INNERMOST,
+                op=ALU.max,
+            )
+            for width in (2, 3):
+                nc.vector.tensor_reduce(
+                    out=top[width][:, chunk, :],
+                    in_=best[width][:, chunk, :].rearrange("c (i n) -> c n i", n=SENTENCES),
+                    axis=INNERMOST,
+                    op=ALU.max,
+                )
+            nc.vector.tensor_reduce(
+                out=top[1][:, chunk, :],
+                in_=conv1_fifths[:, chunk, :].rearrange("c (j n) -> c n j", n=SENTENCES),
+                axis=INNERMOST,
+                op=ALU.max,
+            )
+            nc.vector.tensor_add(top[2][:, chunk, :], top[2][:, chunk, :], top[3][:, chunk, :])
+            nc.vector.tensor_add(top[1][:, chunk, :], top[1][:, chunk, :], top[2][:, chunk, :])
+            nc.tensor.transpose(pooled_flip[:, chunk * P : (chunk + 1) * P], top[1][:, chunk, :], identity[:])
         nc.scalar.activation(out=pooled_sb[:], in_=pooled_flip[:], func=FUNC.Copy, scale=1.0 / len(WIDTHS))
         nc.sync.dma_start(out=pooled[:, :], in_=pooled_sb[:])

@@ -90,16 +90,14 @@ def tile_bertheading_pa_e_kernel(
         make_identity(nc, identity[:])
         nc.gpsimd.memset(minus_half[:], -0.5)
 
-        def load_positions(group):
+        def load_positions(queue, group):
             span = slice(group * GROUP, (group + 1) * GROUP)
-            nc.sync.dma_start(out=x_sb[:, span, :], in_=words_emb[:, span, :])
+            queue.dma_start(out=x_sb[:, span, :], in_=words_emb[:, span, :])
 
-        def load_weight(width):
+        for group in range(AHEAD):
+            load_positions(nc.scalar, group)
+        for width in WIDTHS:
             taps = slice(FIRST_TAP[width], FIRST_TAP[width] + width)
-            nc.sync.dma_start(
-                out=w_codes[:, taps, :].bitcast(I32),
-                in_=weight_words[width].rearrange("g q n t -> q g (n t)").bitcast(I32),
-            )
             for quadrant in range(4):
                 nc.sync.dma_start(
                     out=w_scales[32 * quadrant : 32 * quadrant + 4, taps, :].bitcast(I32),
@@ -107,18 +105,19 @@ def tile_bertheading_pa_e_kernel(
                     .rearrange("g r n -> r g n")
                     .bitcast(I32),
                 )
-
+        for width in WIDTHS:
+            taps = slice(FIRST_TAP[width], FIRST_TAP[width] + width)
+            nc.gpsimd.dma_start(
+                out=w_codes[:, taps, :].bitcast(F32),
+                in_=weight_words[width].rearrange("g q n t -> q g (n t)").bitcast(F32),
+            )
         for width in WIDTHS:
             row = (width - 1) * CHUNKS
             nc.gpsimd.dma_start(
                 out=bias_rows[row : row + CHUNKS, :], in_=biases[width].rearrange("(r c) -> r c", c=P)
             )
-        for group in range(AHEAD):
-            load_positions(group)
-        for width in WIDTHS:
-            load_weight(width)
         for group in range(AHEAD, GROUPS):
-            load_positions(group)
+            load_positions(nc.gpsimd, group)
 
         def bias_of(width, chunk):
             column = (width - 1) * CHUNKS + chunk

@@ -11,7 +11,6 @@ U8 = mybir.dt.uint8
 FP8X4 = mybir.dt.float8_e4m3fn_x4
 ALU = mybir.AluOpType
 FUNC = mybir.ActivationFunctionType
-INNERMOST = mybir.AxisListType.X
 
 P = 128
 SENTENCES = 128
@@ -78,10 +77,7 @@ def tile_bertheading_pa_e_kernel(
             2: keep.tile([P, CHUNKS, GROUP * SENTENCES], F32, name="best2"),
             3: keep.tile([P, CHUNKS, GROUP * SENTENCES], F32, name="best3"),
         }
-        conv1_fifths = keep.tile([P, CHUNKS, GROUPS * SENTENCES], F32, name="conv1_fifths")
-        top = {}
-        for width in WIDTHS:
-            top[width] = keep.tile([P, CHUNKS, SENTENCES], F32, name="top%d" % width)
+        tops = keep.tile([P, 4, FEATURES], F32, name="tops")
         pooled_sb = keep.tile([P, FEATURES], F32, name="pooled_sb")
         out_sb = keep.tile([P, FEATURES, POSITIONS], F32, name="out_sb")
 
@@ -90,14 +86,16 @@ def tile_bertheading_pa_e_kernel(
         make_identity(nc, identity[:])
         nc.gpsimd.memset(minus_half[:], -0.5)
 
-        def load_positions(queue, group):
+        def load_positions(group):
             span = slice(group * GROUP, (group + 1) * GROUP)
-            queue.dma_start(out=x_sb[:, span, :], in_=words_emb[:, span, :])
+            nc.sync.dma_start(out=x_sb[:, span, :], in_=words_emb[:, span, :])
 
-        for group in range(AHEAD):
-            load_positions(nc.scalar, group)
-        for width in WIDTHS:
+        def load_weight(width):
             taps = slice(FIRST_TAP[width], FIRST_TAP[width] + width)
+            nc.sync.dma_start(
+                out=w_codes[:, taps, :].bitcast(I32),
+                in_=weight_words[width].rearrange("g q n t -> q g (n t)").bitcast(I32),
+            )
             for quadrant in range(4):
                 nc.sync.dma_start(
                     out=w_scales[32 * quadrant : 32 * quadrant + 4, taps, :].bitcast(I32),
@@ -105,19 +103,20 @@ def tile_bertheading_pa_e_kernel(
                     .rearrange("g r n -> r g n")
                     .bitcast(I32),
                 )
-        for width in WIDTHS:
-            taps = slice(FIRST_TAP[width], FIRST_TAP[width] + width)
-            nc.gpsimd.dma_start(
-                out=w_codes[:, taps, :].bitcast(F32),
-                in_=weight_words[width].rearrange("g q n t -> q g (n t)").bitcast(F32),
-            )
+
         for width in WIDTHS:
             row = (width - 1) * CHUNKS
             nc.gpsimd.dma_start(
                 out=bias_rows[row : row + CHUNKS, :], in_=biases[width].rearrange("(r c) -> r c", c=P)
             )
+        for group in range(AHEAD):
+            load_positions(group)
+        for width in WIDTHS:
+            load_weight(width)
         for group in range(AHEAD, GROUPS):
-            load_positions(nc.gpsimd, group)
+            load_positions(group)
+
+        nc.gpsimd.memset(tops[:], 0.0)
 
         def bias_of(width, chunk):
             column = (width - 1) * CHUNKS + chunk
@@ -195,14 +194,18 @@ def tile_bertheading_pa_e_kernel(
                         op1=ALU.max,
                     )
 
+        def flip(flipped, values, position):
+            for chunk in range(CHUNKS):
+                nc.tensor.transpose(
+                    flipped[:, chunk * P : (chunk + 1) * P], values[:, chunk, tokens(position, 1)], identity[:]
+                )
+
         def flip_position(group, i, code, by_sentence, sum_squares):
             flipped = flip_banks.tile([P, FEATURES], F32, tag="flip")
-            for chunk in range(CHUNKS):
-                if i < positions_in_group(2, group):
-                    source = code[:, chunk, tokens(i, 1)]
-                else:
-                    source = conv1[:, chunk, tokens(group * GROUP + i, 1)]
-                nc.tensor.transpose(flipped[:, chunk * P : (chunk + 1) * P], source, identity[:])
+            if i < positions_in_group(2, group):
+                flip(flipped, code, i)
+            else:
+                flip(flipped, conv1, group * GROUP + i)
             squares = stage.tile([P, FEATURES], BF16, tag="squares")
             nc.scalar.activation(out=squares[:], in_=flipped[:], func=FUNC.Square, accum_out=sum_squares[:, i : i + 1])
             nc.scalar.copy(out=by_sentence[:, i, :], in_=flipped[:])
@@ -245,34 +248,21 @@ def tile_bertheading_pa_e_kernel(
                     quantise_position((group + AHEAD) * GROUP + step)
             if group > 0:
                 normalise(group - 1, by_sentence[group - 1], sum_squares[group - 1])
+        def take_in(row, values, position):
+            flipped = conv_banks.tile([P, FEATURES], F32, tag="conv")
+            flip(flipped, values, position)
+            nc.vector.tensor_max(tops[:, row, :], flipped[:], tops[:, row, :])
+
         last = GROUPS - 1
         for i in range(GROUP):
             flip_position(last, i, code[last], by_sentence[last], sum_squares[last])
-        normalise(last, by_sentence[last], sum_squares[last])
-
-        pooled_flip = flip_banks.tile([P, FEATURES], F32, tag="flip")
-        for chunk in range(CHUNKS):
-            nc.vector.tensor_reduce(
-                out=conv1_fifths[:, chunk, :].rearrange("c (j n) -> c j n", n=SENTENCES),
-                in_=conv1[:, chunk, :].rearrange("c (i j n) -> c j n i", i=GROUP, n=SENTENCES),
-                axis=INNERMOST,
-                op=ALU.max,
-            )
             for width in (2, 3):
-                nc.vector.tensor_reduce(
-                    out=top[width][:, chunk, :],
-                    in_=best[width][:, chunk, :].rearrange("c (i n) -> c n i", n=SENTENCES),
-                    axis=INNERMOST,
-                    op=ALU.max,
-                )
-            nc.vector.tensor_reduce(
-                out=top[1][:, chunk, :],
-                in_=conv1_fifths[:, chunk, :].rearrange("c (j n) -> c n j", n=SENTENCES),
-                axis=INNERMOST,
-                op=ALU.max,
-            )
-            nc.vector.tensor_add(top[2][:, chunk, :], top[2][:, chunk, :], top[3][:, chunk, :])
-            nc.vector.tensor_add(top[1][:, chunk, :], top[1][:, chunk, :], top[2][:, chunk, :])
-            nc.tensor.transpose(pooled_flip[:, chunk * P : (chunk + 1) * P], top[1][:, chunk, :], identity[:])
-        nc.scalar.activation(out=pooled_sb[:], in_=pooled_flip[:], func=FUNC.Copy, scale=1.0 / len(WIDTHS))
+                take_in(width, best[width], i)
+        normalise(last, by_sentence[last], sum_squares[last])
+        for position in range(POSITIONS):
+            take_in(position % 2, conv1, position)
+        nc.vector.tensor_add(tops[:, 2, :], tops[:, 2, :], tops[:, 3, :])
+        nc.vector.tensor_max(tops[:, 0, :], tops[:, 0, :], tops[:, 1, :])
+        nc.vector.tensor_add(tops[:, 0, :], tops[:, 0, :], tops[:, 2, :])
+        nc.scalar.activation(out=pooled_sb[:], in_=tops[:, 0, :], func=FUNC.Copy, scale=1.0 / len(WIDTHS))
         nc.sync.dma_start(out=pooled[:, :], in_=pooled_sb[:])

@@ -23,7 +23,12 @@ TAPS = sum(WIDTHS)
 CHUNKS = FEATURES // P
 GROUP = 4
 GROUPS = POSITIONS // GROUP
+BANK = GROUP * SENTENCES
 AHEAD = 2
+CODE_ROWS = 2
+CONV1_ROW = CODE_ROWS
+BEST_ROW = {2: CONV1_ROW + GROUPS, 3: CONV1_ROW + GROUPS + 1}
+ROWS = CONV1_ROW + GROUPS + 2
 EPS = 1e-12
 
 FLOPS = 2 * SENTENCES * EMBED * FEATURES * sum(k * (POSITIONS - k + 1) for k in WIDTHS)
@@ -72,11 +77,7 @@ def tile_bertheading_pa_e_kernel(
         bias_rows = keep.tile([P, P], BF16, name="bias_rows")
         bias_rows_f32 = keep.tile([P, P], F32, name="bias_rows_f32")
         bias_cols = keep.tile([P, len(WIDTHS) * CHUNKS], F32, name="bias_cols")
-        conv1 = keep.tile([P, CHUNKS, POSITIONS * SENTENCES], F32, name="conv1")
-        best = {
-            2: keep.tile([P, CHUNKS, GROUP * SENTENCES], F32, name="best2"),
-            3: keep.tile([P, CHUNKS, GROUP * SENTENCES], F32, name="best3"),
-        }
+        state = keep.tile([P, CHUNKS, ROWS, BANK], F32, name="state")
         tops = keep.tile([P, 4, FEATURES], F32, name="tops")
         pooled_sb = keep.tile([P, FEATURES], F32, name="pooled_sb")
         out_sb = keep.tile([P, FEATURES, POSITIONS], F32, name="out_sb")
@@ -152,60 +153,60 @@ def tile_bertheading_pa_e_kernel(
                     )
             return bank
 
-        def convolve_and_fold(group, chunk, code):
+        def two_rows(chunk, upper, lower, cols):
+            return state[:, chunk, upper : lower + 1 : lower - upper, cols]
+
+        def convolve_and_fold(group, chunk):
             banks = {}
             for width in WIDTHS:
                 banks[width] = convolve(width, group, chunk)
+            code_row = group % CODE_ROWS
             nc.scalar.activation(
-                out=conv1[:, chunk, tokens(group * GROUP, GROUP)],
+                out=state[:, chunk, CONV1_ROW + group, :],
                 in_=banks[1][:],
                 func=FUNC.Relu,
                 bias=bias_of(1, chunk),
                 scale=1.0,
             )
             for width in (2, 3):
-                count = positions_in_group(width, group)
-                cols = tokens(0, count)
-                so_far = conv1[:, chunk, tokens(group * GROUP, count)] if width == 2 else code[:, chunk, cols]
+                cols = tokens(0, positions_in_group(width, group))
+                so_far_row = CONV1_ROW + group if width == 2 else code_row
                 if group == 0:
                     nc.scalar.activation(
-                        out=best[width][:, chunk, :],
+                        out=state[:, chunk, BEST_ROW[width], :],
                         in_=banks[width][:],
                         func=FUNC.Relu,
                         bias=bias_of(width, chunk),
                         scale=1.0,
                     )
-                    nc.vector.tensor_max(code[:, chunk, cols], best[width][:, chunk, cols], so_far)
-                else:
-                    nc.vector.scalar_tensor_tensor(
-                        out=code[:, chunk, cols],
-                        in0=banks[width][:, cols],
-                        scalar=bias_of(width, chunk),
-                        in1=so_far,
-                        op0=ALU.add,
-                        op1=ALU.max,
+                    nc.vector.tensor_max(
+                        state[:, chunk, code_row, cols],
+                        state[:, chunk, BEST_ROW[width], cols],
+                        state[:, chunk, so_far_row, cols],
                     )
+                else:
+                    bank = banks[width][:, cols]
                     nc.vector.scalar_tensor_tensor(
-                        out=best[width][:, chunk, cols],
-                        in0=banks[width][:, cols],
+                        out=two_rows(chunk, code_row, BEST_ROW[width], cols),
+                        in0=bank.unsqueeze(1).to_broadcast([P, 2, bank.shape[1]]),
                         scalar=bias_of(width, chunk),
-                        in1=best[width][:, chunk, cols],
+                        in1=two_rows(chunk, so_far_row, BEST_ROW[width], cols),
                         op0=ALU.add,
                         op1=ALU.max,
                     )
 
-        def flip(flipped, values, position):
+        def flip(flipped, row, i):
             for chunk in range(CHUNKS):
                 nc.tensor.transpose(
-                    flipped[:, chunk * P : (chunk + 1) * P], values[:, chunk, tokens(position, 1)], identity[:]
+                    flipped[:, chunk * P : (chunk + 1) * P], state[:, chunk, row, tokens(i, 1)], identity[:]
                 )
 
-        def flip_position(group, i, code, by_sentence, sum_squares):
+        def flip_position(group, i, by_sentence, sum_squares):
             flipped = flip_banks.tile([P, FEATURES], F32, tag="flip")
             if i < positions_in_group(2, group):
-                flip(flipped, code, i)
+                flip(flipped, group % CODE_ROWS, i)
             else:
-                flip(flipped, conv1, group * GROUP + i)
+                flip(flipped, CONV1_ROW + group, i)
             squares = stage.tile([P, FEATURES], BF16, tag="squares")
             nc.scalar.activation(out=squares[:], in_=flipped[:], func=FUNC.Square, accum_out=sum_squares[:, i : i + 1])
             nc.scalar.copy(out=by_sentence[:, i, :], in_=flipped[:])
@@ -233,34 +234,32 @@ def tile_bertheading_pa_e_kernel(
         nc.tensor.transpose(bias_flip[:], bias_rows_f32[:], identity[:])
         nc.vector.tensor_copy(out=bias_cols[:], in_=bias_flip[:, : len(WIDTHS) * CHUNKS])
 
-        code = {}
         by_sentence = {}
         sum_squares = {}
         for group in range(GROUPS):
-            code[group] = stage.tile([P, CHUNKS, GROUP * SENTENCES], F32, tag="code", name="code")
             by_sentence[group] = stage.tile([P, GROUP, FEATURES], F32, tag="by_sentence", name="by_sentence")
             sum_squares[group] = stage.tile([P, GROUP], F32, tag="sum_squares", name="sum_squares")
             for step in range(CHUNKS):
-                convolve_and_fold(group, step, code[group])
+                convolve_and_fold(group, step)
                 if group > 0:
-                    flip_position(group - 1, step, code[group - 1], by_sentence[group - 1], sum_squares[group - 1])
+                    flip_position(group - 1, step, by_sentence[group - 1], sum_squares[group - 1])
                 if group + AHEAD < GROUPS:
                     quantise_position((group + AHEAD) * GROUP + step)
             if group > 0:
                 normalise(group - 1, by_sentence[group - 1], sum_squares[group - 1])
-        def take_in(row, values, position):
+        def take_in(top_row, row, i):
             flipped = conv_banks.tile([P, FEATURES], F32, tag="conv")
-            flip(flipped, values, position)
-            nc.vector.tensor_max(tops[:, row, :], flipped[:], tops[:, row, :])
+            flip(flipped, row, i)
+            nc.vector.tensor_max(tops[:, top_row, :], flipped[:], tops[:, top_row, :])
 
         last = GROUPS - 1
         for i in range(GROUP):
-            flip_position(last, i, code[last], by_sentence[last], sum_squares[last])
+            flip_position(last, i, by_sentence[last], sum_squares[last])
             for width in (2, 3):
-                take_in(width, best[width], i)
+                take_in(width, BEST_ROW[width], i)
         normalise(last, by_sentence[last], sum_squares[last])
         for position in range(POSITIONS):
-            take_in(position % 2, conv1, position)
+            take_in(position % 2, CONV1_ROW + position // GROUP, position % GROUP)
         nc.vector.tensor_add(tops[:, 2, :], tops[:, 2, :], tops[:, 3, :])
         nc.vector.tensor_max(tops[:, 0, :], tops[:, 0, :], tops[:, 1, :])
         nc.vector.tensor_add(tops[:, 0, :], tops[:, 0, :], tops[:, 2, :])

@@ -123,13 +123,19 @@ def tile_bertheading_pa_e_kernel(
             column = (width - 1) * CHUNKS + chunk
             return bias_cols[:, column : column + 1]
 
-        def quantise_position(position):
+        def flip_words(position):
             words = x_sb[:, position, :].bitcast(F32)
             flipped = flip_banks.tile([P, 2, SENTENCES], F32, tag="flip")
             for u in range(2):
                 nc.tensor.transpose(flipped[:, u, :], words[:, u : EMBED // 2 : 2], identity[:])
+            return flipped
+
+        def regroup_words(flipped):
             grouped = stage.tile([P, SENTENCES, 4], BF16, tag="grouped", align_bytes=64)
             nc.scalar.copy(out=grouped[:].bitcast(F32), in_=flipped[:].rearrange("q u n -> q n u"))
+            return grouped
+
+        def quantise_words(position, grouped):
             nc.vector.quantize_mx(
                 out=x_codes[:, tokens(position, 1)].bitcast(FP8X4),
                 scales=x_scales[:, tokens(position, 1)],
@@ -156,29 +162,27 @@ def tile_bertheading_pa_e_kernel(
         def two_rows(chunk, upper, lower, cols):
             return state[:, chunk, upper : lower + 1 : lower - upper, cols]
 
-        def convolve_and_fold(group, chunk):
+        def relu_into(row, chunk, width, bank):
+            nc.scalar.activation(
+                out=state[:, chunk, row, :], in_=bank[:], func=FUNC.Relu, bias=bias_of(width, chunk), scale=1.0
+            )
+
+        def convolve_all(group, chunk):
             banks = {}
             for width in WIDTHS:
                 banks[width] = convolve(width, group, chunk)
+            relu_into(CONV1_ROW + group, chunk, 1, banks[1])
+            if group == 0:
+                for width in (2, 3):
+                    relu_into(BEST_ROW[width], chunk, width, banks[width])
+            return banks
+
+        def fold(group, chunk, banks):
             code_row = group % CODE_ROWS
-            nc.scalar.activation(
-                out=state[:, chunk, CONV1_ROW + group, :],
-                in_=banks[1][:],
-                func=FUNC.Relu,
-                bias=bias_of(1, chunk),
-                scale=1.0,
-            )
             for width in (2, 3):
                 cols = tokens(0, positions_in_group(width, group))
                 so_far_row = CONV1_ROW + group if width == 2 else code_row
                 if group == 0:
-                    nc.scalar.activation(
-                        out=state[:, chunk, BEST_ROW[width], :],
-                        in_=banks[width][:],
-                        func=FUNC.Relu,
-                        bias=bias_of(width, chunk),
-                        scale=1.0,
-                    )
                     nc.vector.tensor_max(
                         state[:, chunk, code_row, cols],
                         state[:, chunk, BEST_ROW[width], cols],
@@ -201,25 +205,36 @@ def tile_bertheading_pa_e_kernel(
                     flipped[:, chunk * P : (chunk + 1) * P], state[:, chunk, row, tokens(i, 1)], identity[:]
                 )
 
-        def flip_position(group, i, by_sentence, sum_squares):
+        by_sentence = {}
+        sum_squares = {}
+
+        def flip_code(group, i):
+            if i == 0:
+                by_sentence[group] = stage.tile([P, GROUP, FEATURES], F32, tag="by_sentence", name="by_sentence")
+                sum_squares[group] = stage.tile([P, GROUP], F32, tag="sum_squares", name="sum_squares")
             flipped = flip_banks.tile([P, FEATURES], F32, tag="flip")
             if i < positions_in_group(2, group):
                 flip(flipped, group % CODE_ROWS, i)
             else:
                 flip(flipped, CONV1_ROW + group, i)
             squares = stage.tile([P, FEATURES], BF16, tag="squares")
-            nc.scalar.activation(out=squares[:], in_=flipped[:], func=FUNC.Square, accum_out=sum_squares[:, i : i + 1])
-            nc.scalar.copy(out=by_sentence[:, i, :], in_=flipped[:])
+            nc.scalar.activation(
+                out=squares[:], in_=flipped[:], func=FUNC.Square, accum_out=sum_squares[group][:, i : i + 1]
+            )
+            return flipped
 
-        def normalise(group, by_sentence, sum_squares):
+        def keep_code(group, i, flipped):
+            nc.scalar.copy(out=by_sentence[group][:, i, :], in_=flipped[:])
+            if i < GROUP - 1:
+                return
             inverse = stage.tile([P, GROUP], F32, tag="inverse")
-            nc.gpsimd.tensor_scalar_max(inverse[:], sum_squares[:], EPS * EPS)
+            nc.gpsimd.tensor_scalar_max(inverse[:], sum_squares[group][:], EPS * EPS)
             nc.gpsimd.tensor_tensor(out=inverse[:], in0=inverse[:], in1=minus_half[:], op=ALU.pow)
             for chunk in range(CHUNKS):
                 features = slice(chunk * P, (chunk + 1) * P)
                 nc.gpsimd.tensor_tensor(
                     out=out_sb[:, features, group * GROUP : (group + 1) * GROUP],
-                    in0=by_sentence[:, :, features].rearrange("n i c -> n c i"),
+                    in0=by_sentence[group][:, :, features].rearrange("n i c -> n c i"),
                     in1=inverse[:].unsqueeze(1).to_broadcast([P, P, GROUP]),
                     op=ALU.mult,
                 )
@@ -227,37 +242,42 @@ def tile_bertheading_pa_e_kernel(
                     nc.sync.dma_start(out=words_out[:, features, :], in_=out_sb[:, features, :])
 
         for position in range(AHEAD * GROUP):
-            quantise_position(position)
+            quantise_words(position, regroup_words(flip_words(position)))
 
         nc.vector.tensor_copy(out=bias_rows_f32[:], in_=bias_rows[:])
         bias_flip = flip_banks.tile([P, P], F32, tag="flip")
         nc.tensor.transpose(bias_flip[:], bias_rows_f32[:], identity[:])
         nc.vector.tensor_copy(out=bias_cols[:], in_=bias_flip[:, : len(WIDTHS) * CHUNKS])
 
-        by_sentence = {}
-        sum_squares = {}
+        code_left = None
+        words_left = None
         for group in range(GROUPS):
-            by_sentence[group] = stage.tile([P, GROUP, FEATURES], F32, tag="by_sentence", name="by_sentence")
-            sum_squares[group] = stage.tile([P, GROUP], F32, tag="sum_squares", name="sum_squares")
             for step in range(CHUNKS):
-                convolve_and_fold(group, step)
-                if group > 0:
-                    flip_position(group - 1, step, by_sentence[group - 1], sum_squares[group - 1])
-                if group + AHEAD < GROUPS:
-                    quantise_position((group + AHEAD) * GROUP + step)
-            if group > 0:
-                normalise(group - 1, by_sentence[group - 1], sum_squares[group - 1])
+                banks = convolve_all(group, step)
+                if code_left:
+                    keep_code(*code_left)
+                grouped = regroup_words(words_left[1]) if words_left else None
+                fold(group, step, banks)
+                if words_left:
+                    quantise_words(words_left[0], grouped)
+                code_left = (group - 1, step, flip_code(group - 1, step)) if group > 0 else None
+                position = (group + AHEAD) * GROUP + step
+                words_left = (position, flip_words(position)) if position < POSITIONS else None
+        keep_code(*code_left)
+
         def take_in(top_row, row, i):
             flipped = conv_banks.tile([P, FEATURES], F32, tag="conv")
             flip(flipped, row, i)
             nc.vector.tensor_max(tops[:, top_row, :], flipped[:], tops[:, top_row, :])
 
         last = GROUPS - 1
+        last_banks = []
         for i in range(GROUP):
-            flip_position(last, i, by_sentence[last], sum_squares[last])
+            last_banks.append(flip_code(last, i))
             for width in (2, 3):
                 take_in(width, BEST_ROW[width], i)
-        normalise(last, by_sentence[last], sum_squares[last])
+        for i in range(GROUP):
+            keep_code(last, i, last_banks[i])
         for position in range(POSITIONS):
             take_in(position % 2, CONV1_ROW + position // GROUP, position % GROUP)
         nc.vector.tensor_add(tops[:, 2, :], tops[:, 2, :], tops[:, 3, :])

@@ -30,6 +30,8 @@ CONV1_ROW = CODE_ROWS
 BEST_ROW = {2: CONV1_ROW + GROUPS, 3: CONV1_ROW + GROUPS + 1}
 ROWS = CONV1_ROW + GROUPS + 2
 EPS = 1e-12
+THIRD = 1.0 / len(WIDTHS)
+LAST = GROUPS - 1
 
 FLOPS = 2 * SENTENCES * EMBED * FEATURES * sum(k * (POSITIONS - k + 1) for k in WIDTHS)
 
@@ -117,7 +119,7 @@ def tile_bertheading_pa_e_kernel(
         for group in range(AHEAD, GROUPS):
             load_positions(group)
 
-        nc.gpsimd.memset(tops[:], 0.0)
+        nc.gpsimd.memset(tops[:, 0:2, :], 0.0)
 
         def bias_of(width, chunk):
             column = (width - 1) * CHUNKS + chunk
@@ -179,6 +181,15 @@ def tile_bertheading_pa_e_kernel(
 
         def fold(group, chunk, banks):
             code_row = group % CODE_ROWS
+            if group == LAST:
+                nc.vector.scalar_tensor_tensor(
+                    out=state[:, chunk, CONV1_ROW + LAST - 1, :],
+                    in0=banks[1][:],
+                    scalar=bias_of(1, chunk),
+                    in1=state[:, chunk, CONV1_ROW + LAST - 1, :],
+                    op0=ALU.add,
+                    op1=ALU.max,
+                )
             for width in (2, 3):
                 cols = tokens(0, positions_in_group(width, group))
                 so_far_row = CONV1_ROW + group if width == 2 else code_row
@@ -223,23 +234,56 @@ def tile_bertheading_pa_e_kernel(
             )
             return flipped
 
+        def invert_norms(sums):
+            inverse = stage.tile([P, GROUP], F32, tag="inverse")
+            nc.gpsimd.tensor_scalar_max(inverse[:], sums, EPS * EPS)
+            nc.gpsimd.tensor_tensor(out=inverse[:], in0=inverse[:], in1=minus_half[:], op=ALU.pow)
+            return inverse
+
+        def features_of(part):
+            return slice(part * P, (part + 1) * P)
+
+        def scale_part(engine, group, part, rows, inverse):
+            engine.tensor_tensor(
+                out=out_sb[:, features_of(part), group * GROUP : (group + 1) * GROUP],
+                in0=rows.rearrange("n i c -> n c i"),
+                in1=inverse[:].unsqueeze(1).to_broadcast([P, P, GROUP]),
+                op=ALU.mult,
+            )
+
+        def scale_group(group, sums):
+            inverse = invert_norms(sums)
+            for part in range(CHUNKS):
+                scale_part(nc.gpsimd, group, part, by_sentence[group][:, :, features_of(part)], inverse)
+                if group == LAST:
+                    nc.sync.dma_start(out=words_out[:, features_of(part), :], in_=out_sb[:, features_of(part), :])
+
         def keep_code(group, i, flipped):
             nc.scalar.copy(out=by_sentence[group][:, i, :], in_=flipped[:])
-            if i < GROUP - 1:
-                return
-            inverse = stage.tile([P, GROUP], F32, tag="inverse")
-            nc.gpsimd.tensor_scalar_max(inverse[:], sum_squares[group][:], EPS * EPS)
-            nc.gpsimd.tensor_tensor(out=inverse[:], in0=inverse[:], in1=minus_half[:], op=ALU.pow)
-            for chunk in range(CHUNKS):
-                features = slice(chunk * P, (chunk + 1) * P)
-                nc.gpsimd.tensor_tensor(
-                    out=out_sb[:, features, group * GROUP : (group + 1) * GROUP],
-                    in0=by_sentence[group][:, :, features].rearrange("n i c -> n c i"),
-                    in1=inverse[:].unsqueeze(1).to_broadcast([P, P, GROUP]),
-                    op=ALU.mult,
+            if i == GROUP - 1:
+                scale_group(group, sum_squares[group][:])
+
+        part_sums = keep.tile([P, GROUP, CHUNKS], F32, name="part_sums")
+
+        def flip_chunk(chunk):
+            if chunk == 0:
+                by_sentence[LAST] = stage.tile([P, GROUP, FEATURES], F32, tag="by_sentence", name="by_sentence")
+            flipped = flip_banks.tile([P, GROUP, P], F32, tag="flip")
+            for i in range(GROUP):
+                row = LAST % CODE_ROWS if i < positions_in_group(2, LAST) else CONV1_ROW + LAST
+                nc.tensor.transpose(flipped[:, i, :], state[:, chunk, row, tokens(i, 1)], identity[:])
+            for i in range(GROUP):
+                squares = stage.tile([P, FEATURES], BF16, tag="squares")
+                nc.scalar.activation(
+                    out=squares[:, :P],
+                    in_=flipped[:, i, :],
+                    func=FUNC.Square,
+                    accum_out=part_sums[:, i, chunk : chunk + 1],
                 )
-                if group == GROUPS - 1:
-                    nc.sync.dma_start(out=words_out[:, features, :], in_=out_sb[:, features, :])
+            return flipped
+
+        def keep_chunk(chunk, flipped):
+            nc.scalar.copy(out=by_sentence[LAST][:, :, features_of(chunk)], in_=flipped[:])
 
         for position in range(AHEAD * GROUP):
             quantise_words(position, regroup_words(flip_words(position)))
@@ -249,39 +293,66 @@ def tile_bertheading_pa_e_kernel(
         nc.tensor.transpose(bias_flip[:], bias_rows_f32[:], identity[:])
         nc.vector.tensor_copy(out=bias_cols[:], in_=bias_flip[:, : len(WIDTHS) * CHUNKS])
 
-        code_left = None
+        def positions_to_flip(group, step):
+            if group == 0:
+                return []
+            if group < LAST:
+                return [(group - 1, step)]
+            return [[(LAST - 1, 0), (LAST - 1, 1)], [(LAST - 1, 2)], [(LAST - 1, 3)], []][step]
+
+        code_left = []
+        chunks_left = []
         words_left = None
         for group in range(GROUPS):
             for step in range(CHUNKS):
                 banks = convolve_all(group, step)
-                if code_left:
-                    keep_code(*code_left)
+                for left in code_left:
+                    keep_code(*left)
                 grouped = regroup_words(words_left[1]) if words_left else None
                 fold(group, step, banks)
                 if words_left:
                     quantise_words(words_left[0], grouped)
-                code_left = (group - 1, step, flip_code(group - 1, step)) if group > 0 else None
+                code_left = [(g, i, flip_code(g, i)) for g, i in positions_to_flip(group, step)]
                 position = (group + AHEAD) * GROUP + step
                 words_left = (position, flip_words(position)) if position < POSITIONS else None
-        keep_code(*code_left)
+        for chunk in range(2):
+            chunks_left.append((chunk, flip_chunk(chunk)))
 
-        def take_in(top_row, row, i):
+        def take_in(top_row, row, i, first):
             flipped = conv_banks.tile([P, FEATURES], F32, tag="conv")
             flip(flipped, row, i)
-            nc.vector.tensor_max(tops[:, top_row, :], flipped[:], tops[:, top_row, :])
+            if first:
+                nc.scalar.activation(out=tops[:, top_row, :], in_=flipped[:], func=FUNC.Copy, scale=THIRD)
+            else:
+                nc.vector.scalar_tensor_tensor(
+                    out=tops[:, top_row, :],
+                    in0=flipped[:],
+                    scalar=THIRD,
+                    in1=tops[:, top_row, :],
+                    op0=ALU.mult,
+                    op1=ALU.max,
+                )
 
-        last = GROUPS - 1
-        last_banks = []
-        for i in range(GROUP):
-            last_banks.append(flip_code(last, i))
-            for width in (2, 3):
-                take_in(width, BEST_ROW[width], i)
-        for i in range(GROUP):
-            keep_code(last, i, last_banks[i])
-        for position in range(POSITIONS):
-            take_in(position % 2, CONV1_ROW + position // GROUP, position % GROUP)
+        conv1_jobs = [(p % 2, CONV1_ROW + p // GROUP, p % GROUP, False) for p in range(LAST * GROUP)]
+        other_jobs = [(width, BEST_ROW[width], i, i == 0) for i in range(GROUP) for width in (2, 3)]
+        jobs = conv1_jobs[: len(conv1_jobs) - len(other_jobs)]
+        for k in range(len(other_jobs)):
+            jobs.extend([other_jobs[k], conv1_jobs[len(conv1_jobs) - len(other_jobs) + k]])
+
+        chunks_left.append((2, flip_chunk(2)))
+        for job in jobs[:2]:
+            take_in(*job)
+        chunks_left.append((3, flip_chunk(3)))
+        for left in chunks_left:
+            keep_chunk(*left)
+        halves = stage.tile([P, GROUP, 2], F32, tag="halves")
+        sums = stage.tile([P, GROUP], F32, tag="sums")
+        nc.gpsimd.tensor_tensor(out=halves[:], in0=part_sums[:, :, 0:2], in1=part_sums[:, :, 2:4], op=ALU.add)
+        nc.gpsimd.tensor_tensor(out=sums[:], in0=halves[:, :, 0], in1=halves[:, :, 1], op=ALU.add)
+        scale_group(LAST, sums[:])
+        for job in jobs[2:]:
+            take_in(*job)
         nc.vector.tensor_add(tops[:, 2, :], tops[:, 2, :], tops[:, 3, :])
         nc.vector.tensor_max(tops[:, 0, :], tops[:, 0, :], tops[:, 1, :])
-        nc.vector.tensor_add(tops[:, 0, :], tops[:, 0, :], tops[:, 2, :])
-        nc.scalar.activation(out=pooled_sb[:], in_=tops[:, 0, :], func=FUNC.Copy, scale=1.0 / len(WIDTHS))
+        nc.vector.tensor_add(pooled_sb[:], tops[:, 0, :], tops[:, 2, :])
         nc.sync.dma_start(out=pooled[:, :], in_=pooled_sb[:])

@@ -112,10 +112,11 @@ def tile_bertheading_pa_e_kernel(
             nc.gpsimd.dma_start(
                 out=bias_rows[row : row + CHUNKS, :], in_=biases[width].rearrange("(r c) -> r c", c=P)
             )
-        for group in range(AHEAD):
-            load_positions(group)
-        for width in WIDTHS:
-            load_weight(width)
+        load_positions(0)
+        load_weight(1)
+        load_positions(1)
+        load_weight(2)
+        load_weight(3)
         for group in range(AHEAD, GROUPS):
             load_positions(group)
 
@@ -132,9 +133,12 @@ def tile_bertheading_pa_e_kernel(
                 nc.tensor.transpose(flipped[:, u, :], words[:, u : EMBED // 2 : 2], identity[:])
             return flipped
 
-        def regroup_words(flipped):
-            grouped = stage.tile([P, SENTENCES, 4], BF16, tag="grouped", align_bytes=64)
-            nc.scalar.copy(out=grouped[:].bitcast(F32), in_=flipped[:].rearrange("q u n -> q n u"))
+        def regroup_words(flipped, on_vector=False):
+            grouped = stage.tile([P, SENTENCES, 4], BF16, tag="grouped", align_bytes=64, bufs=4)
+            if on_vector:
+                nc.vector.tensor_copy(out=grouped[:].bitcast(F32), in_=flipped[:].rearrange("q u n -> q n u"))
+            else:
+                nc.scalar.copy(out=grouped[:].bitcast(F32), in_=flipped[:].rearrange("q u n -> q n u"))
             return grouped
 
         def quantise_words(position, grouped):
@@ -285,13 +289,38 @@ def tile_bertheading_pa_e_kernel(
         def keep_chunk(chunk, flipped):
             nc.scalar.copy(out=by_sentence[LAST][:, :, features_of(chunk)], in_=flipped[:])
 
-        for position in range(AHEAD * GROUP):
+        def prepare_on_vector(positions):
+            flips = [flip_words(position) for position in positions]
+            tiles = [regroup_words(flipped, on_vector=True) for flipped in flips]
+            for k in range(len(positions)):
+                quantise_words(positions[k], tiles[k])
+
+        def first_group(width, chunks):
+            row = CONV1_ROW if width == 1 else BEST_ROW[width]
+            for chunk in chunks:
+                relu_into(row, chunk, width, convolve(width, 0, chunk))
+                if width > 1:
+                    so_far_row = CONV1_ROW if width == 2 else 0
+                    nc.vector.tensor_max(state[:, chunk, 0, :], state[:, chunk, row, :], state[:, chunk, so_far_row, :])
+
+        for position in range(GROUP):
             quantise_words(position, regroup_words(flip_words(position)))
+        conv1_banks = [convolve(1, 0, chunk) for chunk in range(CHUNKS)]
 
         nc.vector.tensor_copy(out=bias_rows_f32[:], in_=bias_rows[:])
         bias_flip = flip_banks.tile([P, P], F32, tag="flip")
         nc.tensor.transpose(bias_flip[:], bias_rows_f32[:], identity[:])
         nc.vector.tensor_copy(out=bias_cols[:], in_=bias_flip[:, : len(WIDTHS) * CHUNKS])
+        for chunk in range(CHUNKS):
+            relu_into(CONV1_ROW, chunk, 1, conv1_banks[chunk])
+
+        prepare_on_vector([4, 5])
+        prepare_on_vector([6, 7])
+        first_group(2, range(CHUNKS))
+        first_group(3, range(2))
+        prepare_on_vector([8, 9])
+        first_group(3, range(2, CHUNKS))
+        prepare_on_vector([10, 11])
 
         def positions_to_flip(group, step):
             if group == 0:
@@ -303,7 +332,7 @@ def tile_bertheading_pa_e_kernel(
         code_left = []
         chunks_left = []
         words_left = None
-        for group in range(GROUPS):
+        for group in range(1, GROUPS):
             for step in range(CHUNKS):
                 banks = convolve_all(group, step)
                 for left in code_left:

@@ -84,8 +84,9 @@ def tile_bertheading_pa_e_kernel(
         pooled_sb = keep.tile([P, FEATURES], F32, name="pooled_sb")
         out_sb = keep.tile([P, FEATURES, POSITIONS], F32, name="out_sb")
 
-        nc.vector.memset(w_scales[:].bitcast(I32), 0)
         nc.vector.memset(bias_rows[:], 0.0)
+        nc.vector.memset(w_scales[:].bitcast(I32), 0)
+        nc.vector.memset(tops[:, 0:2, :], 0.0)
         make_identity(nc, identity[:])
         nc.gpsimd.memset(minus_half[:], -0.5)
 
@@ -107,12 +108,12 @@ def tile_bertheading_pa_e_kernel(
                     .bitcast(I32),
                 )
 
+        load_positions(0)
         for width in WIDTHS:
             row = (width - 1) * CHUNKS
-            nc.gpsimd.dma_start(
+            nc.scalar.dma_start(
                 out=bias_rows[row : row + CHUNKS, :], in_=biases[width].rearrange("(r c) -> r c", c=P)
             )
-        load_positions(0)
         load_weight(1)
         load_positions(1)
         load_weight(2)
@@ -120,7 +121,6 @@ def tile_bertheading_pa_e_kernel(
         for group in range(AHEAD, GROUPS):
             load_positions(group)
 
-        nc.gpsimd.memset(tops[:, 0:2, :], 0.0)
 
         def bias_of(width, chunk):
             column = (width - 1) * CHUNKS + chunk

@@ -32,6 +32,8 @@ ROWS = CONV1_ROW + GROUPS + 2
 EPS = 1e-12
 THIRD = 1.0 / len(WIDTHS)
 LAST = GROUPS - 1
+BEFORE_SCALING = 9
+WARM_UP = 5
 
 FLOPS = 2 * SENTENCES * EMBED * FEATURES * sum(k * (POSITIONS - k + 1) for k in WIDTHS)
 
@@ -259,8 +261,6 @@ def tile_bertheading_pa_e_kernel(
             inverse = invert_norms(sums)
             for part in range(CHUNKS):
                 scale_part(nc.gpsimd, group, part, by_sentence[group][:, :, features_of(part)], inverse)
-                if group == LAST:
-                    nc.sync.dma_start(out=words_out[:, features_of(part), :], in_=out_sb[:, features_of(part), :])
 
         def keep_code(group, i, flipped):
             nc.scalar.copy(out=by_sentence[group][:, i, :], in_=flipped[:])
@@ -270,8 +270,6 @@ def tile_bertheading_pa_e_kernel(
         part_sums = keep.tile([P, GROUP, CHUNKS], F32, name="part_sums")
 
         def flip_chunk(chunk):
-            if chunk == 0:
-                by_sentence[LAST] = stage.tile([P, GROUP, FEATURES], F32, tag="by_sentence", name="by_sentence")
             flipped = flip_banks.tile([P, GROUP, P], F32, tag="flip")
             for i in range(GROUP):
                 row = LAST % CODE_ROWS if i < positions_in_group(2, LAST) else CONV1_ROW + LAST
@@ -285,9 +283,6 @@ def tile_bertheading_pa_e_kernel(
                     accum_out=part_sums[:, i, chunk : chunk + 1],
                 )
             return flipped
-
-        def keep_chunk(chunk, flipped):
-            nc.scalar.copy(out=by_sentence[LAST][:, :, features_of(chunk)], in_=flipped[:])
 
         def prepare_on_vector(positions):
             flips = [flip_words(position) for position in positions]
@@ -303,6 +298,9 @@ def tile_bertheading_pa_e_kernel(
                     so_far_row = CONV1_ROW if width == 2 else 0
                     nc.vector.tensor_max(state[:, chunk, 0, :], state[:, chunk, row, :], state[:, chunk, so_far_row, :])
 
+        warm = conv_banks.tile([P, GROUP * SENTENCES], F32, tag="conv")
+        for k in range(WARM_UP):
+            nc.tensor.matmul(out=warm[:, :P], lhsT=identity[:], rhs=identity[:], start=True, stop=True)
         for position in range(GROUP):
             quantise_words(position, regroup_words(flip_words(position)))
         conv1_banks = [convolve(1, 0, chunk) for chunk in range(CHUNKS)]
@@ -372,14 +370,17 @@ def tile_bertheading_pa_e_kernel(
         for job in jobs[:2]:
             take_in(*job)
         chunks_left.append((3, flip_chunk(3)))
-        for left in chunks_left:
-            keep_chunk(*left)
         halves = stage.tile([P, GROUP, 2], F32, tag="halves")
         sums = stage.tile([P, GROUP], F32, tag="sums")
         nc.gpsimd.tensor_tensor(out=halves[:], in0=part_sums[:, :, 0:2], in1=part_sums[:, :, 2:4], op=ALU.add)
         nc.gpsimd.tensor_tensor(out=sums[:], in0=halves[:, :, 0], in1=halves[:, :, 1], op=ALU.add)
-        scale_group(LAST, sums[:])
-        for job in jobs[2:]:
+        inverse_last = invert_norms(sums[:])
+        for job in jobs[2:BEFORE_SCALING]:
+            take_in(*job)
+        for chunk, flipped in chunks_left:
+            scale_part(nc.vector, LAST, chunk, flipped[:], inverse_last)
+            nc.sync.dma_start(out=words_out[:, features_of(chunk), :], in_=out_sb[:, features_of(chunk), :])
+        for job in jobs[BEFORE_SCALING:]:
             take_in(*job)
         nc.vector.tensor_add(tops[:, 2, :], tops[:, 2, :], tops[:, 3, :])
         nc.vector.tensor_max(tops[:, 0, :], tops[:, 0, :], tops[:, 1, :])

@@ -32,8 +32,11 @@ ROWS = CONV1_ROW + GROUPS + 2
 EPS = 1e-12
 THIRD = 1.0 / len(WIDTHS)
 LAST = GROUPS - 1
-BEFORE_SCALING = 9
+LOOP_T = []
+WORDS = {(1, 0): [10, 12], (1, 1): [14, 16], (2, 0): [18]}
+BEFORE_SCALING = 6
 WARM_UP = 5
+EARLY = 2 * GROUP
 
 FLOPS = 2 * SENTENCES * EMBED * FEATURES * sum(k * (POSITIONS - k + 1) for k in WIDTHS)
 
@@ -83,12 +86,12 @@ def tile_bertheading_pa_e_kernel(
         bias_cols = keep.tile([P, len(WIDTHS) * CHUNKS], F32, name="bias_cols")
         state = keep.tile([P, CHUNKS, ROWS, BANK], F32, name="state")
         tops = keep.tile([P, 4, FEATURES], F32, name="tops")
+        with_bias = keep.tile([P, FEATURES], F32, name="with_bias")
         pooled_sb = keep.tile([P, FEATURES], F32, name="pooled_sb")
         out_sb = keep.tile([P, FEATURES, POSITIONS], F32, name="out_sb")
 
         nc.vector.memset(bias_rows[:], 0.0)
         nc.vector.memset(w_scales[:].bitcast(I32), 0)
-        nc.vector.memset(tops[:, 0:2, :], 0.0)
         make_identity(nc, identity[:])
         nc.gpsimd.memset(minus_half[:], -0.5)
 
@@ -143,6 +146,31 @@ def tile_bertheading_pa_e_kernel(
                 nc.scalar.copy(out=grouped[:].bitcast(F32), in_=flipped[:].rearrange("q u n -> q n u"))
             return grouped
 
+        def flip_pair(position):
+            flipped = flip_banks.tile([P, 2, 2, SENTENCES], F32, tag="flip")
+            for i in range(2):
+                words = x_sb[:, position + i, :].bitcast(F32)
+                for u in range(2):
+                    nc.tensor.transpose(flipped[:, i, u, :], words[:, u : EMBED // 2 : 2], identity[:])
+            return flipped
+
+        def regroup_pair(flipped, on_vector=False):
+            grouped = stage.tile([P, 2 * SENTENCES, 4], BF16, tag="grouped_pair", align_bytes=64, bufs=2)
+            out = grouped[:].rearrange("q (i n) t -> q i (n t)", i=2).bitcast(F32).rearrange("q i (n u) -> q i n u", u=2)
+            source = flipped[:].rearrange("q i u n -> q i n u")
+            if on_vector:
+                nc.vector.tensor_copy(out=out, in_=source)
+            else:
+                nc.scalar.copy(out=out, in_=source)
+            return grouped
+
+        def quantise_pair(position, grouped):
+            nc.vector.quantize_mx(
+                out=x_codes[:, tokens(position, 2)].bitcast(FP8X4),
+                scales=x_scales[:, tokens(position, 2)],
+                in_=grouped[:].rearrange("q n t -> q (n t)"),
+            )
+
         def quantise_words(position, grouped):
             nc.vector.quantize_mx(
                 out=x_codes[:, tokens(position, 1)].bitcast(FP8X4),
@@ -185,36 +213,37 @@ def tile_bertheading_pa_e_kernel(
                     relu_into(BEST_ROW[width], chunk, width, banks[width])
             return banks
 
-        def fold(group, chunk, banks):
+        def fold_rows(chunk, width, bank, cols, out_rows, in_rows):
+            source = bank[:, cols]
+            if len(out_rows) == 1:
+                out = state[:, chunk, out_rows[0], cols]
+                in1 = state[:, chunk, in_rows[0], cols]
+            else:
+                out = two_rows(chunk, out_rows[0], out_rows[1], cols)
+                in1 = two_rows(chunk, in_rows[0], in_rows[1], cols)
+                source = source.unsqueeze(1).to_broadcast([P, 2, source.shape[1]])
+            nc.vector.scalar_tensor_tensor(
+                out=out, in0=source, scalar=bias_of(width, chunk), in1=in1, op0=ALU.add, op1=ALU.max
+            )
+
+        def fold(group, chunk, banks, between=None, code_first=False):
             code_row = group % CODE_ROWS
-            if group == LAST:
-                nc.vector.scalar_tensor_tensor(
-                    out=state[:, chunk, CONV1_ROW + LAST - 1, :],
-                    in0=banks[1][:],
-                    scalar=bias_of(1, chunk),
-                    in1=state[:, chunk, CONV1_ROW + LAST - 1, :],
-                    op0=ALU.add,
-                    op1=ALU.max,
-                )
-            for width in (2, 3):
-                cols = tokens(0, positions_in_group(width, group))
-                so_far_row = CONV1_ROW + group if width == 2 else code_row
-                if group == 0:
-                    nc.vector.tensor_max(
-                        state[:, chunk, code_row, cols],
-                        state[:, chunk, BEST_ROW[width], cols],
-                        state[:, chunk, so_far_row, cols],
-                    )
-                else:
-                    bank = banks[width][:, cols]
-                    nc.vector.scalar_tensor_tensor(
-                        out=two_rows(chunk, code_row, BEST_ROW[width], cols),
-                        in0=bank.unsqueeze(1).to_broadcast([P, 2, bank.shape[1]]),
-                        scalar=bias_of(width, chunk),
-                        in1=two_rows(chunk, so_far_row, BEST_ROW[width], cols),
-                        op0=ALU.add,
-                        op1=ALU.max,
-                    )
+            cols2 = tokens(0, positions_in_group(2, group))
+            cols3 = tokens(0, positions_in_group(3, group))
+            conv1_row = CONV1_ROW + group
+            if code_first:
+                fold_rows(chunk, 2, banks[2], cols2, [code_row], [conv1_row])
+                fold_rows(chunk, 3, banks[3], cols3, [code_row], [code_row])
+                fold_rows(chunk, 2, banks[2], cols2, [BEST_ROW[2]], [BEST_ROW[2]])
+                fold_rows(chunk, 3, banks[3], cols3, [BEST_ROW[3]], [BEST_ROW[3]])
+                return
+            fold_rows(chunk, 2, banks[2], cols2, [code_row, BEST_ROW[2]], [conv1_row, BEST_ROW[2]])
+            if between:
+                between()
+                fold_rows(chunk, 3, banks[3], cols3, [code_row, BEST_ROW[3]], [code_row, BEST_ROW[3]])
+            else:
+                fold_rows(chunk, 3, banks[3], cols3, [BEST_ROW[3]], [BEST_ROW[3]])
+                fold_rows(chunk, 3, banks[3], cols3, [code_row], [code_row])
 
         def flip(flipped, row, i):
             for chunk in range(CHUNKS):
@@ -224,71 +253,101 @@ def tile_bertheading_pa_e_kernel(
 
         by_sentence = {}
         sum_squares = {}
+        inverse = {}
 
         def flip_code(group, i):
             if i == 0:
                 by_sentence[group] = stage.tile([P, GROUP, FEATURES], F32, tag="by_sentence", name="by_sentence")
-                sum_squares[group] = stage.tile([P, GROUP], F32, tag="sum_squares", name="sum_squares")
+            if i % 2 == 0:
+                sum_squares[group, i // 2] = stage.tile([P, 2], F32, tag="sum_squares", name="sum_squares")
             flipped = flip_banks.tile([P, FEATURES], F32, tag="flip")
             if i < positions_in_group(2, group):
                 flip(flipped, group % CODE_ROWS, i)
             else:
                 flip(flipped, CONV1_ROW + group, i)
-            squares = stage.tile([P, FEATURES], BF16, tag="squares")
-            nc.scalar.activation(
-                out=squares[:], in_=flipped[:], func=FUNC.Square, accum_out=sum_squares[group][:, i : i + 1]
-            )
             return flipped
 
+        def square_code(group, i, flipped):
+            squares = stage.tile([P, FEATURES], BF16, tag="squares")
+            pair = sum_squares[group, i // 2]
+            nc.scalar.activation(
+                out=squares[:], in_=flipped[:], func=FUNC.Square, accum_out=pair[:, i % 2 : i % 2 + 1]
+            )
+            if i % 2 == 1:
+                inverse[group, i // 2] = invert_norms(pair[:])
+
         def invert_norms(sums):
-            inverse = stage.tile([P, GROUP], F32, tag="inverse")
-            nc.gpsimd.tensor_scalar_max(inverse[:], sums, EPS * EPS)
-            nc.gpsimd.tensor_tensor(out=inverse[:], in0=inverse[:], in1=minus_half[:], op=ALU.pow)
-            return inverse
+            count = sums.shape[1]
+            inverses = stage.tile([P, count], F32, tag="inverse%d" % count, name="inverses")
+            nc.gpsimd.tensor_scalar_max(inverses[:], sums, EPS * EPS)
+            nc.gpsimd.tensor_tensor(out=inverses[:], in0=inverses[:], in1=minus_half[:, :count], op=ALU.pow)
+            return inverses
 
         def features_of(part):
             return slice(part * P, (part + 1) * P)
 
-        def scale_part(engine, group, part, rows, inverse):
-            engine.tensor_tensor(
-                out=out_sb[:, features_of(part), group * GROUP : (group + 1) * GROUP],
-                in0=rows.rearrange("n i c -> n c i"),
-                in1=inverse[:].unsqueeze(1).to_broadcast([P, P, GROUP]),
-                op=ALU.mult,
-            )
-
-        def scale_group(group, sums):
-            inverse = invert_norms(sums)
+        def interleave_group(group):
             for part in range(CHUNKS):
-                scale_part(nc.gpsimd, group, part, by_sentence[group][:, :, features_of(part)], inverse)
-
-        def keep_code(group, i, flipped):
-            nc.scalar.copy(out=by_sentence[group][:, i, :], in_=flipped[:])
-            if i == GROUP - 1:
-                scale_group(group, sum_squares[group][:])
-
-        part_sums = keep.tile([P, GROUP, CHUNKS], F32, name="part_sums")
-
-        def flip_chunk(chunk):
-            flipped = flip_banks.tile([P, GROUP, P], F32, tag="flip")
-            for i in range(GROUP):
-                row = LAST % CODE_ROWS if i < positions_in_group(2, LAST) else CONV1_ROW + LAST
-                nc.tensor.transpose(flipped[:, i, :], state[:, chunk, row, tokens(i, 1)], identity[:])
-            for i in range(GROUP):
-                squares = stage.tile([P, FEATURES], BF16, tag="squares")
-                nc.scalar.activation(
-                    out=squares[:, :P],
-                    in_=flipped[:, i, :],
-                    func=FUNC.Square,
-                    accum_out=part_sums[:, i, chunk : chunk + 1],
+                nc.gpsimd.tensor_scalar(
+                    out=out_sb[:, features_of(part), group * GROUP : (group + 1) * GROUP],
+                    in0=by_sentence[group][:, :, features_of(part)].rearrange("n i c -> n c i"),
+                    scalar1=1.0,
+                    scalar2=0.0,
+                    op0=ALU.mult,
+                    op1=ALU.add,
                 )
-            return flipped
+                if group == LAST:
+                    nc.sync.dma_start(out=words_out[:, features_of(part), :], in_=out_sb[:, features_of(part), :])
 
-        def prepare_on_vector(positions):
-            flips = [flip_words(position) for position in positions]
-            tiles = [regroup_words(flipped, on_vector=True) for flipped in flips]
-            for k in range(len(positions)):
-                quantise_words(positions[k], tiles[k])
+        def keep_code(group, i, flipped, on_vector=False):
+            out = by_sentence[group][:, i, :]
+            scale = inverse[group, i // 2][:, i % 2 : i % 2 + 1]
+            if on_vector:
+                nc.vector.tensor_scalar_mul(out, flipped[:], scale)
+            else:
+                nc.scalar.activation(out=out, in_=flipped[:], func=FUNC.Copy, scale=scale)
+            if i == GROUP - 1:
+                interleave_group(group)
+
+        def take_in(top_row, bank, first):
+            if first:
+                nc.scalar.activation(out=tops[:, top_row, :], in_=bank[:], func=FUNC.Copy, scale=THIRD)
+            else:
+                nc.vector.scalar_tensor_tensor(
+                    out=tops[:, top_row, :],
+                    in0=bank[:],
+                    scalar=THIRD,
+                    in1=tops[:, top_row, :],
+                    op0=ALU.mult,
+                    op1=ALU.max,
+                )
+
+        def take_in_conv1(position, early=False):
+            if early:
+                bank = flip_banks.tile([P, FEATURES], F32, tag="flip")
+            else:
+                bank = conv_banks.tile([P, FEATURES], F32, tag="conv")
+            nc.tensor.matmul_mx(
+                out=bank[:],
+                lhsT=x_codes[:, tokens(position, 1)].bitcast(FP8X4),
+                lhsT_scale=x_scales[:, tokens(position, 1)],
+                rhs=w_codes[:, FIRST_TAP[1], :].bitcast(FP8X4),
+                rhs_scale=w_scales[:, FIRST_TAP[1], :],
+                start=True,
+                stop=True,
+            )
+            if position < 2:
+                nc.vector.tensor_scalar_mul(tops[:, position, :], bank[:], THIRD)
+            else:
+                take_in(position % 2, bank, False)
+
+        def take_in_best(width, i):
+            bank = conv_banks.tile([P, FEATURES], F32, tag="conv")
+            flip(bank, BEST_ROW[width], i)
+            take_in(width, bank, i == 0)
+
+        def relu_first_group(width, chunk, bank):
+            relu_into(CONV1_ROW if width == 1 else BEST_ROW[width], chunk, width, bank)
 
         def first_group(width, chunks):
             row = CONV1_ROW if width == 1 else BEST_ROW[width]
@@ -301,88 +360,115 @@ def tile_bertheading_pa_e_kernel(
         warm = conv_banks.tile([P, GROUP * SENTENCES], F32, tag="conv")
         for k in range(WARM_UP):
             nc.tensor.matmul(out=warm[:, :P], lhsT=identity[:], rhs=identity[:], start=True, stop=True)
-        for position in range(GROUP):
-            quantise_words(position, regroup_words(flip_words(position)))
-        conv1_banks = [convolve(1, 0, chunk) for chunk in range(CHUNKS)]
-
+        flips = [flip_words(position) for position in range(GROUP)]
+        tiles = [regroup_words(flips[k]) for k in range(GROUP)]
+        for k in range(GROUP):
+            quantise_words(k, tiles[k])
         nc.vector.tensor_copy(out=bias_rows_f32[:], in_=bias_rows[:])
-        bias_flip = flip_banks.tile([P, P], F32, tag="flip")
+        bias_flip = conv_banks.tile([P, P], F32, tag="conv")
         nc.tensor.transpose(bias_flip[:], bias_rows_f32[:], identity[:])
         nc.vector.tensor_copy(out=bias_cols[:], in_=bias_flip[:, : len(WIDTHS) * CHUNKS])
+        conv1_banks = [convolve(1, 0, chunk) for chunk in range(CHUNKS)]
         for chunk in range(CHUNKS):
             relu_into(CONV1_ROW, chunk, 1, conv1_banks[chunk])
 
-        prepare_on_vector([4, 5])
-        prepare_on_vector([6, 7])
+        next_position = [0]
+
+        def next_conv1():
+            take_in_conv1(next_position[0])
+            next_position[0] += 1
+
+        def pair_now(position):
+            quantise_pair(position, regroup_pair(flip_pair(position), on_vector=True))
+
+        pair_now(4)
+        for k in range(3):
+            take_in_conv1(next_position[0], early=True)
+            next_position[0] += 1
         first_group(2, range(CHUNKS))
-        first_group(3, range(2))
-        prepare_on_vector([8, 9])
+        pair_now(6)
+        first_group(3, range(0, 2))
+        pair_now(8)
         first_group(3, range(2, CHUNKS))
-        prepare_on_vector([10, 11])
 
-        def positions_to_flip(group, step):
-            if group == 0:
-                return []
-            if group < LAST:
-                return [(group - 1, step)]
-            return [[(LAST - 1, 0), (LAST - 1, 1)], [(LAST - 1, 2)], [(LAST - 1, 3)], []][step]
 
-        code_left = []
-        chunks_left = []
-        words_left = None
+        def convolve_chunk(group, chunk):
+            banks = {width: convolve(width, group, chunk) for width in WIDTHS}
+            relu_into(CONV1_ROW + group, chunk, 1, banks[1])
+            return banks
+
+        left_codes = []
+        left_words = []
+        to_square = []
         for group in range(1, GROUPS):
-            for step in range(CHUNKS):
-                banks = convolve_all(group, step)
-                for left in code_left:
+            for half in range(2):
+                a, b = 2 * half, 2 * half + 1
+                banks = convolve_chunk(group, a)
+                grouped = [(position, regroup_pair(bank)) for position, bank in left_words]
+                for left in to_square:
+                    square_code(*left)
+                for left in left_codes[: 4 - len(left_codes)]:
                     keep_code(*left)
-                grouped = regroup_words(words_left[1]) if words_left else None
-                fold(group, step, banks)
-                if words_left:
-                    quantise_words(words_left[0], grouped)
-                code_left = [(g, i, flip_code(g, i)) for g, i in positions_to_flip(group, step)]
-                position = (group + AHEAD) * GROUP + step
-                words_left = (position, flip_words(position)) if position < POSITIONS else None
-        for chunk in range(2):
-            chunks_left.append((chunk, flip_chunk(chunk)))
 
-        def take_in(top_row, row, i, first):
-            flipped = conv_banks.tile([P, FEATURES], F32, tag="conv")
-            flip(flipped, row, i)
-            if first:
-                nc.scalar.activation(out=tops[:, top_row, :], in_=flipped[:], func=FUNC.Copy, scale=THIRD)
-            else:
-                nc.vector.scalar_tensor_tensor(
-                    out=tops[:, top_row, :],
-                    in0=flipped[:],
-                    scalar=THIRD,
-                    in1=tops[:, top_row, :],
-                    op0=ALU.mult,
-                    op1=ALU.max,
+                def quantise_left():
+                    for position, tile in grouped:
+                        quantise_pair(position, tile)
+
+                fold(group, a, banks, between=quantise_left if grouped else (next_conv1 if (group, a) in LOOP_T else None))
+                banks = convolve_chunk(group, b)
+                for left in left_codes[4 - len(left_codes) :]:
+                    keep_code(*left)
+                fold(
+                    group,
+                    b,
+                    banks,
+                    between=next_conv1 if (group, b) in LOOP_T else None,
+                    code_first=(group == LAST and half == 1),
                 )
+                left_codes = [(group - 1, i, flip_code(group - 1, i)) for i in ((a, b) if group < LAST else (range(GROUP) if half == 0 else ()))]
+                for left in left_codes[:2]:
+                    square_code(*left)
+                to_square = left_codes[2:]
+                left_words = [(position, flip_pair(position)) for position in WORDS.get((group, half), [])]
 
-        conv1_jobs = [(p % 2, CONV1_ROW + p // GROUP, p % GROUP, False) for p in range(LAST * GROUP)]
-        other_jobs = [(width, BEST_ROW[width], i, i == 0) for i in range(GROUP) for width in (2, 3)]
-        jobs = conv1_jobs[: len(conv1_jobs) - len(other_jobs)]
-        for k in range(len(other_jobs)):
-            jobs.extend([other_jobs[k], conv1_jobs[len(conv1_jobs) - len(other_jobs) + k]])
+        def next_best():
+            take_in_best(*best.pop(0))
 
-        chunks_left.append((2, flip_chunk(2)))
-        for job in jobs[:2]:
-            take_in(*job)
-        chunks_left.append((3, flip_chunk(3)))
-        halves = stage.tile([P, GROUP, 2], F32, tag="halves")
-        sums = stage.tile([P, GROUP], F32, tag="sums")
-        nc.gpsimd.tensor_tensor(out=halves[:], in0=part_sums[:, :, 0:2], in1=part_sums[:, :, 2:4], op=ALU.add)
-        nc.gpsimd.tensor_tensor(out=sums[:], in0=halves[:, :, 0], in1=halves[:, :, 1], op=ALU.add)
-        inverse_last = invert_norms(sums[:])
-        for job in jobs[2:BEFORE_SCALING]:
-            take_in(*job)
-        for chunk, flipped in chunks_left:
-            scale_part(nc.vector, LAST, chunk, flipped[:], inverse_last)
-            nc.sync.dma_start(out=words_out[:, features_of(chunk), :], in_=out_sb[:, features_of(chunk), :])
-        for job in jobs[BEFORE_SCALING:]:
-            take_in(*job)
-        nc.vector.tensor_add(tops[:, 2, :], tops[:, 2, :], tops[:, 3, :])
+        best = [(width, i) for i in range(GROUP) for width in (2, 3)]
+        for k in range(2):
+            next_conv1()
+        codes = [(LAST, i, flip_code(LAST, i)) for i in range(GROUP)]
+        for code in codes:
+            square_code(*code)
+        for k in range(2):
+            next_conv1()
+        for code in codes:
+            keep_code(*code)
+        while next_position[0] < POSITIONS - 4:
+            next_conv1()
+        for k in range(4):
+            next_best()
+        while next_position[0] < POSITIONS:
+            next_conv1()
+        nc_bias = flip_banks.tile([P, FEATURES], F32, tag="flip")
+        for chunk in range(CHUNKS):
+            nc.tensor.matmul(
+                out=nc_bias[:, features_of(chunk)],
+                lhsT=bias_of(1, chunk).to_broadcast([P, P]),
+                rhs=identity[:],
+                start=True,
+                stop=True,
+            )
+        next_best()
         nc.vector.tensor_max(tops[:, 0, :], tops[:, 0, :], tops[:, 1, :])
-        nc.vector.tensor_add(pooled_sb[:], tops[:, 0, :], tops[:, 2, :])
+        next_best()
+        nc.vector.scalar_tensor_tensor(
+            out=with_bias[:], in0=nc_bias[:], scalar=THIRD, in1=tops[:, 0, :], op0=ALU.mult, op1=ALU.add
+        )
+        next_best()
+        next_best()
+        nc.vector.scalar_tensor_tensor(
+            out=tops[:, 2, :], in0=with_bias[:], scalar=0.0, in1=tops[:, 2, :], op0=ALU.max, op1=ALU.add
+        )
+        nc.vector.tensor_add(pooled_sb[:], tops[:, 2, :], tops[:, 3, :])
         nc.sync.dma_start(out=pooled[:, :], in_=pooled_sb[:])

@@ -253,13 +253,11 @@ def tile_bertheading_pa_e_kernel(
 
         by_sentence = {}
         sum_squares = {}
-        inverse = {}
 
         def flip_code(group, i):
             if i == 0:
                 by_sentence[group] = stage.tile([P, GROUP, FEATURES], F32, tag="by_sentence", name="by_sentence")
-            if i % 2 == 0:
-                sum_squares[group, i // 2] = stage.tile([P, 2], F32, tag="sum_squares", name="sum_squares")
+                sum_squares[group] = stage.tile([P, GROUP], F32, tag="sum_squares", name="sum_squares")
             flipped = flip_banks.tile([P, FEATURES], F32, tag="flip")
             if i < positions_in_group(2, group):
                 flip(flipped, group % CODE_ROWS, i)
@@ -269,12 +267,9 @@ def tile_bertheading_pa_e_kernel(
 
         def square_code(group, i, flipped):
             squares = stage.tile([P, FEATURES], BF16, tag="squares")
-            pair = sum_squares[group, i // 2]
             nc.scalar.activation(
-                out=squares[:], in_=flipped[:], func=FUNC.Square, accum_out=pair[:, i % 2 : i % 2 + 1]
+                out=squares[:], in_=flipped[:], func=FUNC.Square, accum_out=sum_squares[group][:, i : i + 1]
             )
-            if i % 2 == 1:
-                inverse[group, i // 2] = invert_norms(pair[:])
 
         def invert_norms(sums):
             count = sums.shape[1]
@@ -286,28 +281,26 @@ def tile_bertheading_pa_e_kernel(
         def features_of(part):
             return slice(part * P, (part + 1) * P)
 
-        def interleave_group(group):
+        def scale_group(group):
+            inverse = invert_norms(sum_squares[group][:])
             for part in range(CHUNKS):
-                nc.gpsimd.tensor_scalar(
+                nc.gpsimd.tensor_tensor(
                     out=out_sb[:, features_of(part), group * GROUP : (group + 1) * GROUP],
                     in0=by_sentence[group][:, :, features_of(part)].rearrange("n i c -> n c i"),
-                    scalar1=1.0,
-                    scalar2=0.0,
-                    op0=ALU.mult,
-                    op1=ALU.add,
+                    in1=inverse[:].unsqueeze(1).to_broadcast([P, P, GROUP]),
+                    op=ALU.mult,
                 )
                 if group == LAST:
                     nc.sync.dma_start(out=words_out[:, features_of(part), :], in_=out_sb[:, features_of(part), :])
 
         def keep_code(group, i, flipped, on_vector=False):
             out = by_sentence[group][:, i, :]
-            scale = inverse[group, i // 2][:, i % 2 : i % 2 + 1]
             if on_vector:
-                nc.vector.tensor_scalar_mul(out, flipped[:], scale)
+                nc.vector.tensor_copy(out=out, in_=flipped[:])
             else:
-                nc.scalar.activation(out=out, in_=flipped[:], func=FUNC.Copy, scale=scale)
+                nc.scalar.copy(out=out, in_=flipped[:])
             if i == GROUP - 1:
-                interleave_group(group)
+                scale_group(group)
 
         def take_in(top_row, bank, first):
             if first:

@@ -33,7 +33,7 @@ EPS = 1e-12
 THIRD = 1.0 / len(WIDTHS)
 LAST = GROUPS - 1
 LOOP_T = []
-WORDS = {(1, 0): [10, 12], (1, 1): [14, 16], (2, 0): [18]}
+WORDS = {(1, 0): [10], (1, 1): [12], (1, 2): [14], (1, 3): [16], (2, 0): [18]}
 BEFORE_SCALING = 6
 WARM_UP = 5
 EARLY = 2 * GROUP
@@ -81,6 +81,7 @@ def tile_bertheading_pa_e_kernel(
         w_scales = keep.tile([P, TAPS, FEATURES], U8, name="w_scales", align_bytes=64)
         identity = keep.tile([P, P], F32, name="identity")
         minus_half = keep.tile([P, GROUP], F32, name="minus_half")
+        eps_squared = keep.tile([P, 2], F32, name="eps_squared")
         bias_rows = keep.tile([P, P], BF16, name="bias_rows")
         bias_rows_f32 = keep.tile([P, P], F32, name="bias_rows_f32")
         bias_cols = keep.tile([P, len(WIDTHS) * CHUNKS], F32, name="bias_cols")
@@ -94,6 +95,13 @@ def tile_bertheading_pa_e_kernel(
         nc.vector.memset(w_scales[:].bitcast(I32), 0)
         make_identity(nc, identity[:])
         nc.gpsimd.memset(minus_half[:], -0.5)
+        nc.gpsimd.memset(eps_squared[:], 1.0)
+        nc.gpsimd.tensor_scalar(
+            out=eps_squared[:, 1:2], in0=eps_squared[:, 0:1], scalar1=EPS * EPS, scalar2=0.0, op0=ALU.mult, op1=ALU.add
+        )
+        nc.gpsimd.tensor_scalar(
+            out=eps_squared[:, 0:1], in0=eps_squared[:, 0:1], scalar1=-EPS * EPS, scalar2=0.0, op0=ALU.mult, op1=ALU.add
+        )
 
         def load_positions(group):
             span = slice(group * GROUP, (group + 1) * GROUP)
@@ -256,7 +264,7 @@ def tile_bertheading_pa_e_kernel(
 
         def flip_code(group, i):
             if i == 0:
-                by_sentence[group] = stage.tile([P, GROUP, FEATURES], F32, tag="by_sentence", name="by_sentence")
+                by_sentence[group] = stage.tile([P, GROUP, FEATURES], F32, tag="by_sentence", name="by_sentence", bufs=3)
                 sum_squares[group] = stage.tile([P, GROUP], F32, tag="sum_squares", name="sum_squares")
             flipped = flip_banks.tile([P, FEATURES], F32, tag="flip")
             if i < positions_in_group(2, group):
@@ -290,8 +298,6 @@ def tile_bertheading_pa_e_kernel(
                     in1=inverse[:].unsqueeze(1).to_broadcast([P, P, GROUP]),
                     op=ALU.mult,
                 )
-                if group == LAST:
-                    nc.sync.dma_start(out=words_out[:, features_of(part), :], in_=out_sb[:, features_of(part), :])
 
         def keep_code(group, i, flipped, on_vector=False):
             out = by_sentence[group][:, i, :]
@@ -301,6 +307,39 @@ def tile_bertheading_pa_e_kernel(
                 nc.scalar.copy(out=out, in_=flipped[:])
             if i == GROUP - 1:
                 scale_group(group)
+
+        def clamp_norms(sums):
+            above = stage.tile([P, 2], F32, tag="above")
+            nc.scalar.activation(out=above[:], in_=sums, func=FUNC.Relu, bias=eps_squared[:, 0:1], scale=1.0)
+            return above
+
+        def invert_clamped(above):
+            inverse = stage.tile([P, 2], F32, tag="last_inverse", bufs=4)
+            nc.scalar.activation(
+                out=inverse[:], in_=above[:], func=FUNC.Abs_reciprocal_sqrt, bias=eps_squared[:, 1:2], scale=1.0
+            )
+            return inverse
+
+        def keep_scaled(group, i, flipped, inverse, on_vector=False):
+            out = by_sentence[group][:, i, :]
+            scale = inverse[:, i % 2 : i % 2 + 1]
+            if on_vector:
+                nc.vector.tensor_scalar_mul(out, flipped[:], scale)
+            else:
+                nc.scalar.activation(out=out, in_=flipped[:], func=FUNC.Copy, scale=scale)
+
+        def interleave(group):
+            for part in range(CHUNKS):
+                nc.gpsimd.tensor_scalar(
+                    out=out_sb[:, features_of(part), group * GROUP : (group + 1) * GROUP],
+                    in0=by_sentence[group][:, :, features_of(part)].rearrange("n i c -> n c i"),
+                    scalar1=1.0,
+                    scalar2=0.0,
+                    op0=ALU.mult,
+                    op1=ALU.add,
+                )
+                if group == LAST:
+                    nc.sync.dma_start(out=words_out[:, features_of(part), :], in_=out_sb[:, features_of(part), :])
 
         def take_in(top_row, bank, first):
             if first:
@@ -392,37 +431,36 @@ def tile_bertheading_pa_e_kernel(
 
         left_codes = []
         left_words = []
-        to_square = []
+        to_keep = []
+        waiting = []
         for group in range(1, GROUPS):
-            for half in range(2):
-                a, b = 2 * half, 2 * half + 1
-                banks = convolve_chunk(group, a)
+            for step in range(CHUNKS):
+                banks = convolve_chunk(group, step)
                 grouped = [(position, regroup_pair(bank)) for position, bank in left_words]
-                for left in to_square:
-                    square_code(*left)
-                for left in left_codes[: 4 - len(left_codes)]:
-                    keep_code(*left)
+                if group < LAST or step == 0:
+                    for left in left_codes:
+                        keep_code(*left)
+                else:
+                    waiting.extend(left_codes)
+                    for code in to_keep:
+                        keep_scaled(*code, on_vector=True)
+                    to_keep = []
+                    while waiting and waiting[-1][1] > waiting[0][1]:
+                        pair = waiting[0][1] // 2
+                        inverse = invert_clamped(clamp_norms(sum_squares[LAST - 1][:, 2 * pair : 2 * pair + 2]))
+                        to_keep = [code + (inverse,) for code in waiting[:2]]
+                        waiting = waiting[2:]
 
                 def quantise_left():
                     for position, tile in grouped:
                         quantise_pair(position, tile)
 
-                fold(group, a, banks, between=quantise_left if grouped else (next_conv1 if (group, a) in LOOP_T else None))
-                banks = convolve_chunk(group, b)
-                for left in left_codes[4 - len(left_codes) :]:
-                    keep_code(*left)
-                fold(
-                    group,
-                    b,
-                    banks,
-                    between=next_conv1 if (group, b) in LOOP_T else None,
-                    code_first=(group == LAST and half == 1),
-                )
-                left_codes = [(group - 1, i, flip_code(group - 1, i)) for i in ((a, b) if group < LAST else (range(GROUP) if half == 0 else ()))]
-                for left in left_codes[:2]:
+                fold(group, step, banks, between=quantise_left if grouped else None, code_first=(group == LAST and step == CHUNKS - 1))
+                wanted = [step] if group < LAST else [[0, 1], [2], [3], []][step]
+                left_codes = [(group - 1, i, flip_code(group - 1, i)) for i in wanted]
+                left_words = [(position, flip_pair(position)) for position in WORDS.get((group, step), [])]
+                for left in left_codes:
                     square_code(*left)
-                to_square = left_codes[2:]
-                left_words = [(position, flip_pair(position)) for position in WORDS.get((group, half), [])]
 
         def next_best():
             take_in_best(*best.pop(0))
@@ -430,13 +468,28 @@ def tile_bertheading_pa_e_kernel(
         best = [(width, i) for i in range(GROUP) for width in (2, 3)]
         for k in range(2):
             next_conv1()
+        for code in to_keep:
+            keep_scaled(*code, on_vector=True)
+        interleave(LAST - 1)
         codes = [(LAST, i, flip_code(LAST, i)) for i in range(GROUP)]
-        for code in codes:
-            square_code(*code)
         for k in range(2):
             next_conv1()
-        for code in codes:
-            keep_code(*code)
+        square_code(*codes[0])
+        square_code(*codes[1])
+        above = clamp_norms(sum_squares[LAST][:, 0:2])
+        square_code(*codes[2])
+        inverses = [invert_clamped(above)]
+        square_code(*codes[3])
+        above = clamp_norms(sum_squares[LAST][:, 2:4])
+
+        keep_scaled(*codes[0], inverses[0])
+        inverses.append(invert_clamped(above))
+        keep_scaled(*codes[1], inverses[0])
+        for k in range(2):
+            next_conv1()
+        for i in range(2, GROUP):
+            keep_scaled(*codes[i], inverses[1], on_vector=True)
+        interleave(LAST)
         while next_position[0] < POSITIONS - 4:
             next_conv1()
         for k in range(4):

@@ -82,8 +82,8 @@ def tile_bertheading_pa_e_kernel(
         identity = keep.tile([P, P], F32, name="identity")
         minus_half = keep.tile([P, GROUP], F32, name="minus_half")
         eps_squared = keep.tile([P, 2], F32, name="eps_squared")
-        bias_rows = keep.tile([P, P], BF16, name="bias_rows")
-        bias_rows_f32 = keep.tile([P, P], F32, name="bias_rows_f32")
+        identity_bf16 = keep.tile([P, P], BF16, name="identity_bf16")
+        bias_rows = keep.tile([P, 2, P], BF16, name="bias_rows")
         bias_cols = keep.tile([P, len(WIDTHS) * CHUNKS], F32, name="bias_cols")
         state = keep.tile([P, CHUNKS, ROWS, BANK], F32, name="state")
         tops = keep.tile([P, 4, FEATURES], F32, name="tops")
@@ -94,6 +94,7 @@ def tile_bertheading_pa_e_kernel(
         nc.vector.memset(bias_rows[:], 0.0)
         nc.vector.memset(w_scales[:].bitcast(I32), 0)
         make_identity(nc, identity[:])
+        nc.gpsimd.tensor_copy(out=identity_bf16[:], in_=identity[:])
         nc.gpsimd.memset(minus_half[:], -0.5)
         nc.gpsimd.memset(eps_squared[:], 1.0)
         nc.gpsimd.tensor_scalar(
@@ -122,18 +123,15 @@ def tile_bertheading_pa_e_kernel(
                 )
 
         load_positions(0)
-        for width in WIDTHS:
-            row = (width - 1) * CHUNKS
-            nc.scalar.dma_start(
-                out=bias_rows[row : row + CHUNKS, :], in_=biases[width].rearrange("(r c) -> r c", c=P)
-            )
+        nc.scalar.dma_start(out=bias_rows[0 : CHUNKS, 0, :], in_=b1.rearrange("(r c) -> r c", c=P))
         load_weight(1)
         load_positions(1)
+        nc.gpsimd.dma_start(out=bias_rows[0 : CHUNKS, 1, :], in_=b2.rearrange("(r c) -> r c", c=P))
+        nc.gpsimd.dma_start(out=bias_rows[CHUNKS : 2 * CHUNKS, 1, :], in_=b3.rearrange("(r c) -> r c", c=P))
         load_weight(2)
         load_weight(3)
-        for group in range(AHEAD, GROUPS):
+        for group in range(2, GROUPS):
             load_positions(group)
-
 
         def bias_of(width, chunk):
             column = (width - 1) * CHUNKS + chunk
@@ -392,14 +390,23 @@ def tile_bertheading_pa_e_kernel(
         warm = conv_banks.tile([P, GROUP * SENTENCES], F32, tag="conv")
         for k in range(WARM_UP):
             nc.tensor.matmul(out=warm[:, :P], lhsT=identity[:], rhs=identity[:], start=True, stop=True)
+        def bias_columns(part, first, count, pool, tag):
+            flipped = pool.tile([P, P], BF16, tag=tag)
+            nc.tensor.transpose(flipped[:], bias_rows[:, part, :], identity_bf16[:])
+            return flipped, first, count
+
+        def keep_columns(flipped, first, count):
+            nc.vector.tensor_copy(out=bias_cols[:, first : first + count], in_=flipped[:, :count])
+
         flips = [flip_words(position) for position in range(GROUP)]
-        tiles = [regroup_words(flips[k]) for k in range(GROUP)]
-        for k in range(GROUP):
+        b1_flip = bias_columns(0, 0, CHUNKS, conv_banks, "conv")
+        tiles = [regroup_words(flips[k], on_vector=(k % 2 == 1)) for k in range(2)]
+        quantise_words(0, tiles[0])
+        tiles.extend([regroup_words(flips[k], on_vector=(k % 2 == 1)) for k in range(2, GROUP)])
+        for k in range(1, GROUP):
             quantise_words(k, tiles[k])
-        nc.vector.tensor_copy(out=bias_rows_f32[:], in_=bias_rows[:])
-        bias_flip = conv_banks.tile([P, P], F32, tag="conv")
-        nc.tensor.transpose(bias_flip[:], bias_rows_f32[:], identity[:])
-        nc.vector.tensor_copy(out=bias_cols[:], in_=bias_flip[:, : len(WIDTHS) * CHUNKS])
+            if k == 2:
+                keep_columns(*b1_flip)
         conv1_banks = [convolve(1, 0, chunk) for chunk in range(CHUNKS)]
         for chunk in range(CHUNKS):
             relu_into(CONV1_ROW, chunk, 1, conv1_banks[chunk])
@@ -414,6 +421,7 @@ def tile_bertheading_pa_e_kernel(
             quantise_pair(position, regroup_pair(flip_pair(position), on_vector=True))
 
         pair_now(4)
+        keep_columns(*bias_columns(1, CHUNKS, 2 * CHUNKS, flip_banks, "flip"))
         for k in range(3):
             take_in_conv1(next_position[0], early=True)
             next_position[0] += 1
@@ -436,6 +444,8 @@ def tile_bertheading_pa_e_kernel(
         for group in range(1, GROUPS):
             for step in range(CHUNKS):
                 banks = convolve_chunk(group, step)
+                for left in left_codes[1:]:
+                    square_code(*left)
                 grouped = [(position, regroup_pair(bank)) for position, bank in left_words]
                 if group < LAST or step == 0:
                     for left in left_codes:
@@ -459,20 +469,23 @@ def tile_bertheading_pa_e_kernel(
                 wanted = [step] if group < LAST else [[0, 1], [2], [3], []][step]
                 left_codes = [(group - 1, i, flip_code(group - 1, i)) for i in wanted]
                 left_words = [(position, flip_pair(position)) for position in WORDS.get((group, step), [])]
-                for left in left_codes:
+                for left in left_codes[:1]:
                     square_code(*left)
 
         def next_best():
             take_in_best(*best.pop(0))
 
         best = [(width, i) for i in range(GROUP) for width in (2, 3)]
-        for k in range(2):
+        for k in range(0):
             next_conv1()
         for code in to_keep:
             keep_scaled(*code, on_vector=True)
         interleave(LAST - 1)
-        codes = [(LAST, i, flip_code(LAST, i)) for i in range(GROUP)]
+        codes = [(LAST, i, flip_code(LAST, i)) for i in range(2)]
         for k in range(2):
+            next_conv1()
+        codes.extend([(LAST, i, flip_code(LAST, i)) for i in range(2, GROUP)])
+        for k in range(0):
             next_conv1()
         square_code(*codes[0])
         square_code(*codes[1])
@@ -484,11 +497,8 @@ def tile_bertheading_pa_e_kernel(
 
         keep_scaled(*codes[0], inverses[0])
         inverses.append(invert_clamped(above))
-        keep_scaled(*codes[1], inverses[0])
-        for k in range(2):
-            next_conv1()
-        for i in range(2, GROUP):
-            keep_scaled(*codes[i], inverses[1], on_vector=True)
+        for i in range(1, GROUP):
+            keep_scaled(*codes[i], inverses[i // 2])
         interleave(LAST)
         while next_position[0] < POSITIONS - 4:
             next_conv1()

@@ -82,6 +82,7 @@ def tile_bertheading_pa_e_kernel(
         identity = keep.tile([P, P], F32, name="identity")
         minus_half = keep.tile([P, GROUP], F32, name="minus_half")
         eps_squared = keep.tile([P, 2], F32, name="eps_squared")
+        table_loader = keep.tile([P, 1], F32, name="table_loader")
         identity_bf16 = keep.tile([P, P], BF16, name="identity_bf16")
         bias_rows = keep.tile([P, 2, P], BF16, name="bias_rows")
         bias_cols = keep.tile([P, len(WIDTHS) * CHUNKS], F32, name="bias_cols")
@@ -91,6 +92,7 @@ def tile_bertheading_pa_e_kernel(
         pooled_sb = keep.tile([P, FEATURES], F32, name="pooled_sb")
         out_sb = keep.tile([P, FEATURES, POSITIONS], F32, name="out_sb")
 
+        nc.vector.memset(table_loader[:], 1.0)
         nc.vector.memset(bias_rows[:], 0.0)
         nc.vector.memset(w_scales[:].bitcast(I32), 0)
         make_identity(nc, identity[:])
@@ -132,6 +134,8 @@ def tile_bertheading_pa_e_kernel(
         load_weight(3)
         for group in range(2, GROUPS):
             load_positions(group)
+
+        nc.scalar.activation(out=table_loader[:], in_=table_loader[:], func=FUNC.Abs_reciprocal_sqrt)
 
         def bias_of(width, chunk):
             column = (width - 1) * CHUNKS + chunk
@@ -240,6 +244,8 @@ def tile_bertheading_pa_e_kernel(
             if code_first:
                 fold_rows(chunk, 2, banks[2], cols2, [code_row], [conv1_row])
                 fold_rows(chunk, 3, banks[3], cols3, [code_row], [code_row])
+                if between:
+                    between()
                 fold_rows(chunk, 2, banks[2], cols2, [BEST_ROW[2]], [BEST_ROW[2]])
                 fold_rows(chunk, 3, banks[3], cols3, [BEST_ROW[3]], [BEST_ROW[3]])
                 return
@@ -261,7 +267,7 @@ def tile_bertheading_pa_e_kernel(
         sum_squares = {}
 
         def flip_code(group, i):
-            if i == 0:
+            if group not in by_sentence:
                 by_sentence[group] = stage.tile([P, GROUP, FEATURES], F32, tag="by_sentence", name="by_sentence", bufs=3)
                 sum_squares[group] = stage.tile([P, GROUP], F32, tag="sum_squares", name="sum_squares")
             flipped = flip_banks.tile([P, FEATURES], F32, tag="flip")
@@ -465,7 +471,14 @@ def tile_bertheading_pa_e_kernel(
                     for position, tile in grouped:
                         quantise_pair(position, tile)
 
-                fold(group, step, banks, between=quantise_left if grouped else None, code_first=(group == LAST and step == CHUNKS - 1))
+                def keep_waiting():
+                    for code in to_keep:
+                        keep_scaled(*code, on_vector=True)
+
+                if group == LAST and step == CHUNKS - 1:
+                    fold(group, step, banks, between=keep_waiting, code_first=True)
+                else:
+                    fold(group, step, banks, between=quantise_left if grouped else None)
                 wanted = [step] if group < LAST else [[0, 1], [2], [3], []][step]
                 left_codes = [(group - 1, i, flip_code(group - 1, i)) for i in wanted]
                 left_words = [(position, flip_pair(position)) for position in WORDS.get((group, step), [])]
@@ -478,27 +491,24 @@ def tile_bertheading_pa_e_kernel(
         best = [(width, i) for i in range(GROUP) for width in (2, 3)]
         for k in range(0):
             next_conv1()
-        for code in to_keep:
-            keep_scaled(*code, on_vector=True)
         interleave(LAST - 1)
-        codes = [(LAST, i, flip_code(LAST, i)) for i in range(2)]
+        codes = {i: (LAST, i, flip_code(LAST, i)) for i in (3, 2)}
         for k in range(2):
             next_conv1()
-        codes.extend([(LAST, i, flip_code(LAST, i)) for i in range(2, GROUP)])
-        for k in range(0):
-            next_conv1()
-        square_code(*codes[0])
-        square_code(*codes[1])
-        above = clamp_norms(sum_squares[LAST][:, 0:2])
-        square_code(*codes[2])
-        inverses = [invert_clamped(above)]
+        for i in range(2):
+            codes[i] = (LAST, i, flip_code(LAST, i))
         square_code(*codes[3])
+        square_code(*codes[2])
         above = clamp_norms(sum_squares[LAST][:, 2:4])
-
-        keep_scaled(*codes[0], inverses[0])
-        inverses.append(invert_clamped(above))
-        for i in range(1, GROUP):
-            keep_scaled(*codes[i], inverses[i // 2])
+        square_code(*codes[0])
+        inverse = invert_clamped(above)
+        square_code(*codes[1])
+        keep_scaled(*codes[3], inverse)
+        above = clamp_norms(sum_squares[LAST][:, 0:2])
+        keep_scaled(*codes[2], inverse)
+        inverse = invert_clamped(above)
+        keep_scaled(*codes[0], inverse)
+        keep_scaled(*codes[1], inverse)
         interleave(LAST)
         while next_position[0] < POSITIONS - 4:
             next_conv1()

@@ -324,16 +324,16 @@ def tile_bertheading_pa_e_kernel(
             )
             return inverse
 
-        def keep_scaled(group, i, flipped, inverse, on_vector=False):
-            out = by_sentence[group][:, i, :]
+        def keep_scaled(group, i, flipped, inverse, features=slice(0, FEATURES), on_vector=False):
+            out = by_sentence[group][:, i, features]
             scale = inverse[:, i % 2 : i % 2 + 1]
             if on_vector:
                 nc.vector.tensor_scalar_mul(out, flipped[:], scale)
             else:
-                nc.scalar.activation(out=out, in_=flipped[:], func=FUNC.Copy, scale=scale)
+                nc.scalar.activation(out=out, in_=flipped[:, features], func=FUNC.Copy, scale=scale)
 
-        def interleave(group):
-            for part in range(CHUNKS):
+        def interleave(group, parts):
+            for part in parts:
                 nc.gpsimd.tensor_scalar(
                     out=out_sb[:, features_of(part), group * GROUP : (group + 1) * GROUP],
                     in0=by_sentence[group][:, :, features_of(part)].rearrange("n i c -> n c i"),
@@ -394,8 +394,12 @@ def tile_bertheading_pa_e_kernel(
                     nc.vector.tensor_max(state[:, chunk, 0, :], state[:, chunk, row, :], state[:, chunk, so_far_row, :])
 
         warm = conv_banks.tile([P, GROUP * SENTENCES], F32, tag="conv")
-        for k in range(WARM_UP):
-            nc.tensor.matmul(out=warm[:, :P], lhsT=identity[:], rhs=identity[:], start=True, stop=True)
+
+        def warm_up(count):
+            for k in range(count):
+                nc.tensor.matmul(out=warm[:, :P], lhsT=identity[:], rhs=identity[:], start=True, stop=True)
+
+        warm_up(WARM_UP)
         def bias_columns(part, first, count, pool, tag):
             flipped = pool.tile([P, P], BF16, tag=tag)
             nc.tensor.transpose(flipped[:], bias_rows[:, part, :], identity_bf16[:])
@@ -406,6 +410,7 @@ def tile_bertheading_pa_e_kernel(
 
         flips = [flip_words(position) for position in range(GROUP)]
         b1_flip = bias_columns(0, 0, CHUNKS, conv_banks, "conv")
+        warm_up(3)
         tiles = [regroup_words(flips[k], on_vector=(k % 2 == 1)) for k in range(2)]
         quantise_words(0, tiles[0])
         tiles.extend([regroup_words(flips[k], on_vector=(k % 2 == 1)) for k in range(2, GROUP)])
@@ -491,7 +496,7 @@ def tile_bertheading_pa_e_kernel(
         best = [(width, i) for i in range(GROUP) for width in (2, 3)]
         for k in range(0):
             next_conv1()
-        interleave(LAST - 1)
+        interleave(LAST - 1, range(3))
         codes = {i: (LAST, i, flip_code(LAST, i)) for i in (3, 2)}
         for k in range(2):
             next_conv1()
@@ -503,38 +508,43 @@ def tile_bertheading_pa_e_kernel(
         square_code(*codes[0])
         inverse = invert_clamped(above)
         square_code(*codes[1])
-        keep_scaled(*codes[3], inverse)
+        halves = [slice(0, FEATURES // 2), slice(FEATURES // 2, FEATURES)]
+        inverses = {2: inverse, 3: inverse}
+        keep_scaled(*codes[3], inverses[3], halves[0])
         above = clamp_norms(sum_squares[LAST][:, 0:2])
-        keep_scaled(*codes[2], inverse)
-        inverse = invert_clamped(above)
-        keep_scaled(*codes[0], inverse)
-        keep_scaled(*codes[1], inverse)
-        interleave(LAST)
-        while next_position[0] < POSITIONS - 4:
+        keep_scaled(*codes[2], inverses[2], halves[0])
+        inverses[0] = inverses[1] = invert_clamped(above)
+        for i in range(2):
+            keep_scaled(*codes[i], inverses[i], halves[0])
+        interleave(LAST, range(CHUNKS // 2))
+        interleave(LAST - 1, range(3, CHUNKS))
+        for i in (3, 2, 0, 1):
+            keep_scaled(*codes[i], inverses[i], halves[1])
+        interleave(LAST, range(CHUNKS // 2, CHUNKS))
+        while next_position[0] < POSITIONS - 5:
             next_conv1()
-        for k in range(4):
+        while best:
             next_best()
+        nc.gpsimd.tensor_tensor(out=tops[:, 2, :], in0=tops[:, 2, :], in1=tops[:, 3, :], op=ALU.add)
         while next_position[0] < POSITIONS:
             next_conv1()
-        nc_bias = flip_banks.tile([P, FEATURES], F32, tag="flip")
+        b1_bank = flip_banks.tile([P, FEATURES], F32, tag="flip")
         for chunk in range(CHUNKS):
             nc.tensor.matmul(
-                out=nc_bias[:, features_of(chunk)],
+                out=b1_bank[:, features_of(chunk)],
                 lhsT=bias_of(1, chunk).to_broadcast([P, P]),
                 rhs=identity[:],
                 start=True,
                 stop=True,
             )
-        next_best()
-        nc.vector.tensor_max(tops[:, 0, :], tops[:, 0, :], tops[:, 1, :])
-        next_best()
-        nc.vector.scalar_tensor_tensor(
-            out=with_bias[:], in0=nc_bias[:], scalar=THIRD, in1=tops[:, 0, :], op0=ALU.mult, op1=ALU.add
-        )
-        next_best()
-        next_best()
-        nc.vector.scalar_tensor_tensor(
-            out=tops[:, 2, :], in0=with_bias[:], scalar=0.0, in1=tops[:, 2, :], op0=ALU.max, op1=ALU.add
-        )
-        nc.vector.tensor_add(pooled_sb[:], tops[:, 2, :], tops[:, 3, :])
+        for half in halves:
+            nc.vector.tensor_max(tops[:, 0, half], tops[:, 0, half], tops[:, 1, half])
+        for half in halves:
+            nc.vector.scalar_tensor_tensor(
+                out=with_bias[:, half], in0=b1_bank[:, half], scalar=THIRD, in1=tops[:, 0, half], op0=ALU.mult, op1=ALU.add
+            )
+        for half in halves:
+            nc.vector.scalar_tensor_tensor(
+                out=pooled_sb[:, half], in0=with_bias[:, half], scalar=0.0, in1=tops[:, 2, half], op0=ALU.max, op1=ALU.add
+            )
         nc.sync.dma_start(out=pooled[:, :], in_=pooled_sb[:])

@@ -35,7 +35,7 @@ LAST = GROUPS - 1
 LOOP_T = []
 WORDS = {(1, 0): [10], (1, 1): [12], (1, 2): [14], (1, 3): [16], (2, 0): [18]}
 BEFORE_SCALING = 6
-WARM_UP = 5
+WARM_UP = 3
 EARLY = 2 * GROUP
 
 FLOPS = 2 * SENTENCES * EMBED * FEATURES * sum(k * (POSITIONS - k + 1) for k in WIDTHS)
@@ -93,8 +93,9 @@ def tile_bertheading_pa_e_kernel(
         out_sb = keep.tile([P, FEATURES, POSITIONS], F32, name="out_sb")
 
         nc.vector.memset(table_loader[:], 1.0)
+        nc.vector.memset(w_scales[:, 0, :].bitcast(I32), 0)
         nc.vector.memset(bias_rows[:], 0.0)
-        nc.vector.memset(w_scales[:].bitcast(I32), 0)
+        nc.vector.memset(w_scales[:, 1:, :].bitcast(I32), 0)
         make_identity(nc, identity[:])
         nc.gpsimd.tensor_copy(out=identity_bf16[:], in_=identity[:])
         nc.gpsimd.memset(minus_half[:], -0.5)
@@ -110,12 +111,15 @@ def tile_bertheading_pa_e_kernel(
             span = slice(group * GROUP, (group + 1) * GROUP)
             nc.sync.dma_start(out=x_sb[:, span, :], in_=words_emb[:, span, :])
 
-        def load_weight(width):
+        def load_words(width):
             taps = slice(FIRST_TAP[width], FIRST_TAP[width] + width)
             nc.sync.dma_start(
                 out=w_codes[:, taps, :].bitcast(I32),
                 in_=weight_words[width].rearrange("g q n t -> q g (n t)").bitcast(I32),
             )
+
+        def load_scales(width):
+            taps = slice(FIRST_TAP[width], FIRST_TAP[width] + width)
             for quadrant in range(4):
                 nc.sync.dma_start(
                     out=w_scales[32 * quadrant : 32 * quadrant + 4, taps, :].bitcast(I32),
@@ -124,18 +128,20 @@ def tile_bertheading_pa_e_kernel(
                     .bitcast(I32),
                 )
 
-        load_positions(0)
+        nc.sync.dma_start(out=x_sb[:, 0:2, :], in_=words_emb[:, 0:2, :])
         nc.scalar.dma_start(out=bias_rows[0 : CHUNKS, 0, :], in_=b1.rearrange("(r c) -> r c", c=P))
-        load_weight(1)
+        load_scales(1)
+        nc.sync.dma_start(out=x_sb[:, 2:4, :], in_=words_emb[:, 2:4, :])
+        load_words(1)
+        nc.scalar.activation(out=table_loader[:], in_=table_loader[:], func=FUNC.Abs_reciprocal_sqrt)
         load_positions(1)
-        nc.gpsimd.dma_start(out=bias_rows[0 : CHUNKS, 1, :], in_=b2.rearrange("(r c) -> r c", c=P))
-        nc.gpsimd.dma_start(out=bias_rows[CHUNKS : 2 * CHUNKS, 1, :], in_=b3.rearrange("(r c) -> r c", c=P))
-        load_weight(2)
-        load_weight(3)
+        nc.scalar.dma_start(out=bias_rows[0 : CHUNKS, 1, :], in_=b2.rearrange("(r c) -> r c", c=P))
+        nc.scalar.dma_start(out=bias_rows[CHUNKS : 2 * CHUNKS, 1, :], in_=b3.rearrange("(r c) -> r c", c=P))
+        for width in (2, 3):
+            load_words(width)
+            load_scales(width)
         for group in range(2, GROUPS):
             load_positions(group)
-
-        nc.scalar.activation(out=table_loader[:], in_=table_loader[:], func=FUNC.Abs_reciprocal_sqrt)
 
         def bias_of(width, chunk):
             column = (width - 1) * CHUNKS + chunk
@@ -470,6 +476,10 @@ def tile_bertheading_pa_e_kernel(
                         pair = waiting[0][1] // 2
                         inverse = invert_clamped(clamp_norms(sum_squares[LAST - 1][:, 2 * pair : 2 * pair + 2]))
                         to_keep = [code + (inverse,) for code in waiting[:2]]
+                        if pair == 1:
+                            for code in to_keep[:1]:
+                                keep_scaled(*code)
+                            to_keep = to_keep[1:]
                         waiting = waiting[2:]
 
                 def quantise_left():

from contextlib import ExitStack

import concourse.mybir as mybir
from concourse.masks import make_identity

F32 = mybir.dt.float32
BF16 = mybir.dt.bfloat16
I32 = mybir.dt.int32
U32 = mybir.dt.uint32
U8 = mybir.dt.uint8
FP8X4 = mybir.dt.float8_e4m3fn_x4
ALU = mybir.AluOpType
FUNC = mybir.ActivationFunctionType

P = 128
SENTENCES = 128
POSITIONS = 20
EMBED = 512
FEATURES = 512
WIDTHS = (1, 2, 3)
FIRST_TAP = {1: 0, 2: 1, 3: 3}
TAPS = sum(WIDTHS)
CHUNKS = FEATURES // P
GROUP = 4
GROUPS = POSITIONS // GROUP
BANK = GROUP * SENTENCES
AHEAD = 2
CODE_ROWS = 2
CONV1_ROW = CODE_ROWS
BEST_ROW = {2: CONV1_ROW + GROUPS, 3: CONV1_ROW + GROUPS + 1}
ROWS = CONV1_ROW + GROUPS + 2
EPS = 1e-12
THIRD = 1.0 / len(WIDTHS)
LAST = GROUPS - 1
LOOP_T = []
WORDS = {(1, 0): [10], (1, 1): [12], (1, 2): [14], (1, 3): [16], (2, 0): [18]}
BEFORE_SCALING = 6
WARM_UP = 3
EARLY = 2 * GROUP

FLOPS = 2 * SENTENCES * EMBED * FEATURES * sum(k * (POSITIONS - k + 1) for k in WIDTHS)


def tokens(first_position, count):
    return slice(first_position * SENTENCES, (first_position + count) * SENTENCES)


def positions_in_group(width, group):
    return min(GROUP, POSITIONS - width + 1 - group * GROUP)


def moving_pieces(count):
    pieces = []
    first = 0
    for size in (4, 2, 1):
        if count - first >= size:
            pieces.append((first, size))
            first += size
    return pieces


def tile_bertheading_pa_e_kernel(
    tc, words_emb, W1_words, W1_scales, b1, W2_words, W2_scales, b2, W3_words, W3_scales, b3, words_out, pooled
):
    nc = tc.nc
    weight_words = {1: W1_words, 2: W2_words, 3: W3_words}
    weight_scales = {1: W1_scales, 2: W2_scales, 3: W3_scales}
    biases = {1: b1, 2: b2, 3: b3}

    with ExitStack() as ctx:
        ctx.enter_context(tc.manual_schedule())
        keep = ctx.enter_context(tc.tile_pool(name="keep", bufs=1))
        stage = ctx.enter_context(tc.tile_pool(name="stage", bufs=2))
        conv_banks = ctx.enter_context(tc.psum_pool(name="conv_banks", bufs=4))
        flip_banks = ctx.enter_context(tc.psum_pool(name="flip_banks", bufs=4))

        x_sb = keep.tile([P, POSITIONS, EMBED], BF16, name="x_sb")
        x_codes = keep.tile([P, POSITIONS * SENTENCES], U32, name="x_codes", align_bytes=64)
        x_scales = keep.tile([P, POSITIONS * SENTENCES], U8, name="x_scales", align_bytes=64)
        w_codes = keep.tile([P, TAPS, FEATURES], U32, name="w_codes", align_bytes=64)
        w_scales = keep.tile([P, TAPS, FEATURES], U8, name="w_scales", align_bytes=64)
        identity = keep.tile([P, P], F32, name="identity")
        minus_half = keep.tile([P, GROUP], F32, name="minus_half")
        eps_squared = keep.tile([P, 2], F32, name="eps_squared")
        table_loader = keep.tile([P, 1], F32, name="table_loader")
        identity_bf16 = keep.tile([P, P], BF16, name="identity_bf16")
        bias_rows = keep.tile([P, 2, P], BF16, name="bias_rows")
        bias_cols = keep.tile([P, len(WIDTHS) * CHUNKS], F32, name="bias_cols")
        state = keep.tile([P, CHUNKS, ROWS, BANK], F32, name="state")
        tops = keep.tile([P, 4, FEATURES], F32, name="tops")
        with_bias = keep.tile([P, FEATURES], F32, name="with_bias")
        pooled_sb = keep.tile([P, FEATURES], F32, name="pooled_sb")
        out_sb = keep.tile([P, FEATURES, POSITIONS], F32, name="out_sb")

        nc.vector.memset(table_loader[:], 1.0)
        nc.vector.memset(w_scales[:, 0, :].bitcast(I32), 0)
        nc.vector.memset(bias_rows[:], 0.0)
        nc.vector.memset(w_scales[:, 1:, :].bitcast(I32), 0)
        make_identity(nc, identity[:])
        nc.gpsimd.tensor_copy(out=identity_bf16[:], in_=identity[:])
        nc.gpsimd.memset(minus_half[:], -0.5)
        nc.gpsimd.memset(eps_squared[:], 1.0)
        nc.gpsimd.tensor_scalar(
            out=eps_squared[:, 1:2], in0=eps_squared[:, 0:1], scalar1=EPS * EPS, scalar2=0.0, op0=ALU.mult, op1=ALU.add
        )
        nc.gpsimd.tensor_scalar(
            out=eps_squared[:, 0:1], in0=eps_squared[:, 0:1], scalar1=-EPS * EPS, scalar2=0.0, op0=ALU.mult, op1=ALU.add
        )

        def load_positions(group):
            span = slice(group * GROUP, (group + 1) * GROUP)
            nc.sync.dma_start(out=x_sb[:, span, :], in_=words_emb[:, span, :])

        def load_words(width):
            taps = slice(FIRST_TAP[width], FIRST_TAP[width] + width)
            nc.sync.dma_start(
                out=w_codes[:, taps, :].bitcast(I32),
                in_=weight_words[width].rearrange("g q n t -> q g (n t)").bitcast(I32),
            )

        def load_scales(width):
            taps = slice(FIRST_TAP[width], FIRST_TAP[width] + width)
            for quadrant in range(4):
                nc.sync.dma_start(
                    out=w_scales[32 * quadrant : 32 * quadrant + 4, taps, :].bitcast(I32),
                    in_=weight_scales[width][:, 4 * quadrant : 4 * quadrant + 4, :]
                    .rearrange("g r n -> r g n")
                    .bitcast(I32),
                )

        nc.sync.dma_start(out=x_sb[:, 0:2, :], in_=words_emb[:, 0:2, :])
        nc.scalar.dma_start(out=bias_rows[0 : CHUNKS, 0, :], in_=b1.rearrange("(r c) -> r c", c=P))
        load_scales(1)
        nc.sync.dma_start(out=x_sb[:, 2:4, :], in_=words_emb[:, 2:4, :])
        load_words(1)
        nc.scalar.activation(out=table_loader[:], in_=table_loader[:], func=FUNC.Abs_reciprocal_sqrt)
        load_positions(1)
        nc.scalar.dma_start(out=bias_rows[0 : CHUNKS, 1, :], in_=b2.rearrange("(r c) -> r c", c=P))
        nc.scalar.dma_start(out=bias_rows[CHUNKS : 2 * CHUNKS, 1, :], in_=b3.rearrange("(r c) -> r c", c=P))
        for width in (2, 3):
            load_words(width)
            load_scales(width)
        for group in range(2, GROUPS):
            load_positions(group)

        def bias_of(width, chunk):
            column = (width - 1) * CHUNKS + chunk
            return bias_cols[:, column : column + 1]

        def flip_words(position):
            words = x_sb[:, position, :].bitcast(F32)
            flipped = flip_banks.tile([P, 2, SENTENCES], F32, tag="flip")
            for u in range(2):
                nc.tensor.transpose(flipped[:, u, :], words[:, u : EMBED // 2 : 2], identity[:])
            return flipped

        def regroup_words(flipped, on_vector=False):
            grouped = stage.tile([P, SENTENCES, 4], BF16, tag="grouped", align_bytes=64, bufs=4)
            if on_vector:
                nc.vector.tensor_copy(out=grouped[:].bitcast(F32), in_=flipped[:].rearrange("q u n -> q n u"))
            else:
                nc.scalar.copy(out=grouped[:].bitcast(F32), in_=flipped[:].rearrange("q u n -> q n u"))
            return grouped

        def flip_pair(position):
            flipped = flip_banks.tile([P, 2, 2, SENTENCES], F32, tag="flip")
            for i in range(2):
                words = x_sb[:, position + i, :].bitcast(F32)
                for u in range(2):
                    nc.tensor.transpose(flipped[:, i, u, :], words[:, u : EMBED // 2 : 2], identity[:])
            return flipped

        def regroup_pair(flipped, on_vector=False):
            grouped = stage.tile([P, 2 * SENTENCES, 4], BF16, tag="grouped_pair", align_bytes=64, bufs=2)
            out = grouped[:].rearrange("q (i n) t -> q i (n t)", i=2).bitcast(F32).rearrange("q i (n u) -> q i n u", u=2)
            source = flipped[:].rearrange("q i u n -> q i n u")
            if on_vector:
                nc.vector.tensor_copy(out=out, in_=source)
            else:
                nc.scalar.copy(out=out, in_=source)
            return grouped

        def quantise_pair(position, grouped):
            nc.vector.quantize_mx(
                out=x_codes[:, tokens(position, 2)].bitcast(FP8X4),
                scales=x_scales[:, tokens(position, 2)],
                in_=grouped[:].rearrange("q n t -> q (n t)"),
            )

        def quantise_words(position, grouped):
            nc.vector.quantize_mx(
                out=x_codes[:, tokens(position, 1)].bitcast(FP8X4),
                scales=x_scales[:, tokens(position, 1)],
                in_=grouped[:].rearrange("q n t -> q (n t)"),
            )

        def convolve(width, group, chunk):
            bank = conv_banks.tile([P, GROUP * SENTENCES], F32, tag="conv")
            features = slice(chunk * P, (chunk + 1) * P)
            for first, size in moving_pieces(positions_in_group(width, group)):
                for tap in range(width):
                    shifted = tokens(group * GROUP + first + tap, size)
                    nc.tensor.matmul_mx(
                        out=bank[:, tokens(first, size)],
                        lhsT=w_codes[:, FIRST_TAP[width] + tap, features].bitcast(FP8X4),
                        lhsT_scale=w_scales[:, FIRST_TAP[width] + tap, features],
                        rhs=x_codes[:, shifted].bitcast(FP8X4),
                        rhs_scale=x_scales[:, shifted],
                        start=(tap == 0),
                        stop=(tap == width - 1),
                    )
            return bank

        def two_rows(chunk, upper, lower, cols):
            return state[:, chunk, upper : lower + 1 : lower - upper, cols]

        def relu_into(row, chunk, width, bank):
            nc.scalar.activation(
                out=state[:, chunk, row, :], in_=bank[:], func=FUNC.Relu, bias=bias_of(width, chunk), scale=1.0
            )

        def convolve_all(group, chunk):
            banks = {}
            for width in WIDTHS:
                banks[width] = convolve(width, group, chunk)
            relu_into(CONV1_ROW + group, chunk, 1, banks[1])
            if group == 0:
                for width in (2, 3):
                    relu_into(BEST_ROW[width], chunk, width, banks[width])
            return banks

        def fold_rows(chunk, width, bank, cols, out_rows, in_rows):
            source = bank[:, cols]
            if len(out_rows) == 1:
                out = state[:, chunk, out_rows[0], cols]
                in1 = state[:, chunk, in_rows[0], cols]
            else:
                out = two_rows(chunk, out_rows[0], out_rows[1], cols)
                in1 = two_rows(chunk, in_rows[0], in_rows[1], cols)
                source = source.unsqueeze(1).to_broadcast([P, 2, source.shape[1]])
            nc.vector.scalar_tensor_tensor(
                out=out, in0=source, scalar=bias_of(width, chunk), in1=in1, op0=ALU.add, op1=ALU.max
            )

        def fold(group, chunk, banks, between=None, code_first=False):
            code_row = group % CODE_ROWS
            cols2 = tokens(0, positions_in_group(2, group))
            cols3 = tokens(0, positions_in_group(3, group))
            conv1_row = CONV1_ROW + group
            if code_first:
                fold_rows(chunk, 2, banks[2], cols2, [code_row], [conv1_row])
                fold_rows(chunk, 3, banks[3], cols3, [code_row], [code_row])
                if between:
                    between()
                fold_rows(chunk, 2, banks[2], cols2, [BEST_ROW[2]], [BEST_ROW[2]])
                fold_rows(chunk, 3, banks[3], cols3, [BEST_ROW[3]], [BEST_ROW[3]])
                return
            fold_rows(chunk, 2, banks[2], cols2, [code_row, BEST_ROW[2]], [conv1_row, BEST_ROW[2]])
            if between:
                between()
                fold_rows(chunk, 3, banks[3], cols3, [code_row, BEST_ROW[3]], [code_row, BEST_ROW[3]])
            else:
                fold_rows(chunk, 3, banks[3], cols3, [BEST_ROW[3]], [BEST_ROW[3]])
                fold_rows(chunk, 3, banks[3], cols3, [code_row], [code_row])

        def flip(flipped, row, i):
            for chunk in range(CHUNKS):
                nc.tensor.transpose(
                    flipped[:, chunk * P : (chunk + 1) * P], state[:, chunk, row, tokens(i, 1)], identity[:]
                )

        by_sentence = {}
        sum_squares = {}

        def flip_code(group, i):
            if group not in by_sentence:
                by_sentence[group] = stage.tile([P, GROUP, FEATURES], F32, tag="by_sentence", name="by_sentence", bufs=3)
                sum_squares[group] = stage.tile([P, GROUP], F32, tag="sum_squares", name="sum_squares")
            flipped = flip_banks.tile([P, FEATURES], F32, tag="flip")
            if i < positions_in_group(2, group):
                flip(flipped, group % CODE_ROWS, i)
            else:
                flip(flipped, CONV1_ROW + group, i)
            return flipped

        def square_code(group, i, flipped):
            squares = stage.tile([P, FEATURES], BF16, tag="squares")
            nc.scalar.activation(
                out=squares[:], in_=flipped[:], func=FUNC.Square, accum_out=sum_squares[group][:, i : i + 1]
            )

        def invert_norms(sums):
            count = sums.shape[1]
            inverses = stage.tile([P, count], F32, tag="inverse%d" % count, name="inverses")
            nc.gpsimd.tensor_scalar_max(inverses[:], sums, EPS * EPS)
            nc.gpsimd.tensor_tensor(out=inverses[:], in0=inverses[:], in1=minus_half[:, :count], op=ALU.pow)
            return inverses

        def features_of(part):
            return slice(part * P, (part + 1) * P)

        def scale_group(group):
            inverse = invert_norms(sum_squares[group][:])
            for part in range(CHUNKS):
                nc.gpsimd.tensor_tensor(
                    out=out_sb[:, features_of(part), group * GROUP : (group + 1) * GROUP],
                    in0=by_sentence[group][:, :, features_of(part)].rearrange("n i c -> n c i"),
                    in1=inverse[:].unsqueeze(1).to_broadcast([P, P, GROUP]),
                    op=ALU.mult,
                )

        def keep_code(group, i, flipped, on_vector=False):
            out = by_sentence[group][:, i, :]
            if on_vector:
                nc.vector.tensor_copy(out=out, in_=flipped[:])
            else:
                nc.scalar.copy(out=out, in_=flipped[:])
            if i == GROUP - 1:
                scale_group(group)

        def clamp_norms(sums):
            above = stage.tile([P, 2], F32, tag="above")
            nc.scalar.activation(out=above[:], in_=sums, func=FUNC.Relu, bias=eps_squared[:, 0:1], scale=1.0)
            return above

        def invert_clamped(above):
            inverse = stage.tile([P, 2], F32, tag="last_inverse", bufs=4)
            nc.scalar.activation(
                out=inverse[:], in_=above[:], func=FUNC.Abs_reciprocal_sqrt, bias=eps_squared[:, 1:2], scale=1.0
            )
            return inverse

        def keep_scaled(group, i, flipped, inverse, features=slice(0, FEATURES), on_vector=False):
            out = by_sentence[group][:, i, features]
            scale = inverse[:, i % 2 : i % 2 + 1]
            if on_vector:
                nc.vector.tensor_scalar_mul(out, flipped[:], scale)
            else:
                nc.scalar.activation(out=out, in_=flipped[:, features], func=FUNC.Copy, scale=scale)

        def interleave(group, parts):
            for part in parts:
                nc.gpsimd.tensor_scalar(
                    out=out_sb[:, features_of(part), group * GROUP : (group + 1) * GROUP],
                    in0=by_sentence[group][:, :, features_of(part)].rearrange("n i c -> n c i"),
                    scalar1=1.0,
                    scalar2=0.0,
                    op0=ALU.mult,
                    op1=ALU.add,
                )
                if group == LAST:
                    nc.sync.dma_start(out=words_out[:, features_of(part), :], in_=out_sb[:, features_of(part), :])

        def take_in(top_row, bank, first):
            if first:
                nc.scalar.activation(out=tops[:, top_row, :], in_=bank[:], func=FUNC.Copy, scale=THIRD)
            else:
                nc.vector.scalar_tensor_tensor(
                    out=tops[:, top_row, :],
                    in0=bank[:],
                    scalar=THIRD,
                    in1=tops[:, top_row, :],
                    op0=ALU.mult,
                    op1=ALU.max,
                )

        def take_in_conv1(position, early=False):
            if early:
                bank = flip_banks.tile([P, FEATURES], F32, tag="flip")
            else:
                bank = conv_banks.tile([P, FEATURES], F32, tag="conv")
            nc.tensor.matmul_mx(
                out=bank[:],
                lhsT=x_codes[:, tokens(position, 1)].bitcast(FP8X4),
                lhsT_scale=x_scales[:, tokens(position, 1)],
                rhs=w_codes[:, FIRST_TAP[1], :].bitcast(FP8X4),
                rhs_scale=w_scales[:, FIRST_TAP[1], :],
                start=True,
                stop=True,
            )
            if position < 2:
                nc.vector.tensor_scalar_mul(tops[:, position, :], bank[:], THIRD)
            else:
                take_in(position % 2, bank, False)

        def take_in_best(width, i):
            bank = conv_banks.tile([P, FEATURES], F32, tag="conv")
            flip(bank, BEST_ROW[width], i)
            take_in(width, bank, i == 0)

        def relu_first_group(width, chunk, bank):
            relu_into(CONV1_ROW if width == 1 else BEST_ROW[width], chunk, width, bank)

        def first_group(width, chunks):
            row = CONV1_ROW if width == 1 else BEST_ROW[width]
            for chunk in chunks:
                relu_into(row, chunk, width, convolve(width, 0, chunk))
                if width > 1:
                    so_far_row = CONV1_ROW if width == 2 else 0
                    nc.vector.tensor_max(state[:, chunk, 0, :], state[:, chunk, row, :], state[:, chunk, so_far_row, :])

        warm = conv_banks.tile([P, GROUP * SENTENCES], F32, tag="conv")

        def warm_up(count):
            for k in range(count):
                nc.tensor.matmul(out=warm[:, :P], lhsT=identity[:], rhs=identity[:], start=True, stop=True)

        warm_up(WARM_UP)
        def bias_columns(part, first, count, pool, tag):
            flipped = pool.tile([P, P], BF16, tag=tag)
            nc.tensor.transpose(flipped[:], bias_rows[:, part, :], identity_bf16[:])
            return flipped, first, count

        def keep_columns(flipped, first, count):
            nc.vector.tensor_copy(out=bias_cols[:, first : first + count], in_=flipped[:, :count])

        flips = [flip_words(position) for position in range(GROUP)]
        b1_flip = bias_columns(0, 0, CHUNKS, conv_banks, "conv")
        warm_up(3)
        tiles = [regroup_words(flips[k], on_vector=(k % 2 == 1)) for k in range(2)]
        quantise_words(0, tiles[0])
        tiles.extend([regroup_words(flips[k], on_vector=(k % 2 == 1)) for k in range(2, GROUP)])
        for k in range(1, GROUP):
            quantise_words(k, tiles[k])
            if k == 2:
                keep_columns(*b1_flip)
        conv1_banks = [convolve(1, 0, chunk) for chunk in range(CHUNKS)]
        for chunk in range(CHUNKS):
            relu_into(CONV1_ROW, chunk, 1, conv1_banks[chunk])

        next_position = [0]

        def next_conv1():
            take_in_conv1(next_position[0])
            next_position[0] += 1

        def pair_now(position):
            quantise_pair(position, regroup_pair(flip_pair(position), on_vector=True))

        pair_now(4)
        keep_columns(*bias_columns(1, CHUNKS, 2 * CHUNKS, flip_banks, "flip"))
        for k in range(3):
            take_in_conv1(next_position[0], early=True)
            next_position[0] += 1
        first_group(2, range(CHUNKS))
        pair_now(6)
        first_group(3, range(0, 2))
        pair_now(8)
        first_group(3, range(2, CHUNKS))


        def convolve_chunk(group, chunk):
            banks = {width: convolve(width, group, chunk) for width in WIDTHS}
            relu_into(CONV1_ROW + group, chunk, 1, banks[1])
            return banks

        left_codes = []
        left_words = []
        to_keep = []
        waiting = []
        for group in range(1, GROUPS):
            for step in range(CHUNKS):
                banks = convolve_chunk(group, step)
                for left in left_codes[1:]:
                    square_code(*left)
                grouped = [(position, regroup_pair(bank)) for position, bank in left_words]
                if group < LAST or step == 0:
                    for left in left_codes:
                        keep_code(*left)
                else:
                    waiting.extend(left_codes)
                    for code in to_keep:
                        keep_scaled(*code, on_vector=True)
                    to_keep = []
                    while waiting and waiting[-1][1] > waiting[0][1]:
                        pair = waiting[0][1] // 2
                        inverse = invert_clamped(clamp_norms(sum_squares[LAST - 1][:, 2 * pair : 2 * pair + 2]))
                        to_keep = [code + (inverse,) for code in waiting[:2]]
                        if pair == 1:
                            for code in to_keep[:1]:
                                keep_scaled(*code)
                            to_keep = to_keep[1:]
                        waiting = waiting[2:]

                def quantise_left():
                    for position, tile in grouped:
                        quantise_pair(position, tile)

                def keep_waiting():
                    for code in to_keep:
                        keep_scaled(*code, on_vector=True)

                if group == LAST and step == CHUNKS - 1:
                    fold(group, step, banks, between=keep_waiting, code_first=True)
                else:
                    fold(group, step, banks, between=quantise_left if grouped else None)
                wanted = [step] if group < LAST else [[0, 1], [2], [3], []][step]
                left_codes = [(group - 1, i, flip_code(group - 1, i)) for i in wanted]
                left_words = [(position, flip_pair(position)) for position in WORDS.get((group, step), [])]
                for left in left_codes[:1]:
                    square_code(*left)

        def next_best():
            take_in_best(*best.pop(0))

        best = [(width, i) for i in range(GROUP) for width in (2, 3)]
        for k in range(0):
            next_conv1()
        interleave(LAST - 1, range(3))
        codes = {i: (LAST, i, flip_code(LAST, i)) for i in (3, 2)}
        for k in range(2):
            next_conv1()
        for i in range(2):
            codes[i] = (LAST, i, flip_code(LAST, i))
        square_code(*codes[3])
        square_code(*codes[2])
        above = clamp_norms(sum_squares[LAST][:, 2:4])
        square_code(*codes[0])
        inverse = invert_clamped(above)
        square_code(*codes[1])
        halves = [slice(0, FEATURES // 2), slice(FEATURES // 2, FEATURES)]
        inverses = {2: inverse, 3: inverse}
        keep_scaled(*codes[3], inverses[3], halves[0])
        above = clamp_norms(sum_squares[LAST][:, 0:2])
        keep_scaled(*codes[2], inverses[2], halves[0])
        inverses[0] = inverses[1] = invert_clamped(above)
        for i in range(2):
            keep_scaled(*codes[i], inverses[i], halves[0])
        interleave(LAST, range(CHUNKS // 2))
        interleave(LAST - 1, range(3, CHUNKS))
        for i in (3, 2, 0, 1):
            keep_scaled(*codes[i], inverses[i], halves[1])
        interleave(LAST, range(CHUNKS // 2, CHUNKS))
        while next_position[0] < POSITIONS - 5:
            next_conv1()
        while best:
            next_best()
        nc.gpsimd.tensor_tensor(out=tops[:, 2, :], in0=tops[:, 2, :], in1=tops[:, 3, :], op=ALU.add)
        while next_position[0] < POSITIONS:
            next_conv1()
        b1_bank = flip_banks.tile([P, FEATURES], F32, tag="flip")
        for chunk in range(CHUNKS):
            nc.tensor.matmul(
                out=b1_bank[:, features_of(chunk)],
                lhsT=bias_of(1, chunk).to_broadcast([P, P]),
                rhs=identity[:],
                start=True,
                stop=True,
            )
        for half in halves:
            nc.vector.tensor_max(tops[:, 0, half], tops[:, 0, half], tops[:, 1, half])
        for half in halves:
            nc.vector.scalar_tensor_tensor(
                out=with_bias[:, half], in0=b1_bank[:, half], scalar=THIRD, in1=tops[:, 0, half], op0=ALU.mult, op1=ALU.add
            )
        for half in halves:
            nc.vector.scalar_tensor_tensor(
                out=pooled_sb[:, half], in0=with_bias[:, half], scalar=0.0, in1=tops[:, 2, half], op0=ALU.max, op1=ALU.add
            )
        nc.sync.dma_start(out=pooled[:, :], in_=pooled_sb[:])
